import numpy as np
import ml_dtypes


def mxq(x, axis, fmt="e4m3"):
    dtype, down = {"e4m3": (ml_dtypes.float8_e4m3fn, 7), "e5m2": (ml_dtypes.float8_e5m2, 14)}[fmt]
    v = np.moveaxis(np.asarray(x, np.float32).astype(ml_dtypes.bfloat16).astype(np.float64), axis, -1)
    blocks = v.reshape(v.shape[:-1] + (-1, 32))
    amax = np.abs(blocks).max(-1, keepdims=True)
    byte = np.maximum(np.where(amax > 0, np.frexp(amax)[1] - 1 + 127, 0) - down, 1)
    scale = np.exp2(byte - 127.0)
    codes = (blocks / scale).astype(np.float32).astype(dtype).astype(np.float64)
    return np.moveaxis((codes * scale).reshape(v.shape), -1, axis)


WIDE = False


def mx_kscale(k):
    if not WIDE:
        return np.ones(k)
    levels = np.array([10, -10, 5, -5, 0])
    a = np.random.permutation(np.resize(levels, k // 512 * 4)).reshape(k // 512, 4)
    idx = np.arange(k)
    return np.exp2(a[idx // 512, idx % 128 // 32])


BF16 = ml_dtypes.bfloat16


def bf(x):
    return np.asarray(x, np.float32).astype(BF16)


def f64(x):
    return np.asarray(x).astype(np.float64)


B, N, D, K = 8, 2048, 512, 128

BN_EPS = 1e-5
NORM_EPS = 1e-12


def _l2_normalize(v, axis):
    n = np.sqrt(np.sum(v * v, axis=axis, keepdims=True))
    return v / np.maximum(n, NORM_EPS)


def setup_inputs():
    s = mx_kscale(D)
    mu = np.random.standard_normal(D) * 0.125
    h = np.random.standard_normal(K)
    return {"x": bf((np.random.standard_normal((B, N, D)) + mu) * s),
            "clusters": bf((np.random.standard_normal((D, K)) * 0.5 / np.sqrt(D) + mu[:, None] * h * 0.25 / np.sum(mu * mu)) / s[:, None]),
            "clusters2": bf((mu[:, None] + np.random.standard_normal((1, D, K)) / np.sqrt(D)) * s[:, None]),
            "bn_gamma": bf(1.0 + 0.1 * np.random.standard_normal(K)),
            "bn_beta": bf(0.5 * np.random.standard_normal(K))}


def reference(x, clusters, clusters2, bn_gamma, bn_beta):
    x, clusters, clusters2 = f64(x), f64(clusters), f64(clusters2)
    bn_gamma, bn_beta = f64(bn_gamma), f64(bn_beta)
    B, N, D = x.shape
    K = clusters2.shape[-1]
    x_flat = x.reshape(-1, D)
    assignment = mxq(x_flat, 1, "e4m3") @ mxq(clusters, 0, "e4m3")
    mean = np.mean(assignment, axis=0)
    var = np.var(assignment, axis=0)
    assignment = (assignment - mean) * (1.0 / np.sqrt(var + BN_EPS)) * bn_gamma + bn_beta
    e = np.exp(assignment - assignment.max(axis=1, keepdims=True))
    assignment = (e / e.sum(axis=1, keepdims=True))[:, :K]
    assignment = assignment.reshape(B, N, K)
    a_sum = np.sum(assignment, axis=1, keepdims=True)
    a = a_sum * clusters2
    vlad = (mxq(x, 1, "e4m3").transpose(0, 2, 1) @ mxq(assignment, 1, "e4m3")) - a
    vlad = _l2_normalize(vlad, axis=1)
    vlad = vlad.reshape(B, D * K)
    vlad = _l2_normalize(vlad, axis=1)
    return vlad

@@ -1,0 +1,358 @@
+from contextlib import ExitStack
+
+import concourse.mybir as mybir
+from concourse.masks import make_identity
+
+F32 = mybir.dt.float32
+BF16 = mybir.dt.bfloat16
+U32 = mybir.dt.uint32
+U8 = mybir.dt.uint8
+FP8X4 = mybir.dt.float8_e4m3fn_x4
+ALU = mybir.AluOpType
+ACT = mybir.ActivationFunctionType
+AX = mybir.AxisListType
+
+P = 128
+PACK = 4
+K_PASS = P * PACK
+B, N, D, K = 8, 2048, 512, 128
+ROWS = B * N
+CHUNKS = ROWS // K_PASS
+CHUNKS_PER_BATCH = N // K_PASS
+D_BLOCKS = D // P
+BN_EPS = 1e-5
+NORM_EPS = 1e-12
+SCALAR_D = 256
+LOAD_AHEAD = 4
+SETUP_STEP = 2
+
+FLOPS = 2 * 2 * ROWS * D * K
+
+
+def live(c):
+    return 0 <= c < CHUNKS
+
+
+def tile_modelnew_kernel(tc, x, clusters, clusters2, bn_gamma, bn_beta, out):
+    nc = tc.nc
+    x_rows = x.flatten_outer_dims()
+
+    with ExitStack() as ctx:
+        ctx.enter_context(tc.manual_schedule())
+        keep = ctx.enter_context(tc.tile_pool(name="keep", bufs=1))
+
+        ident_f32 = keep.tile([P, P], F32)
+        make_identity(nc, ident_f32[:])
+        ident_bf16 = keep.tile([P, P], BF16)
+        make_identity(nc, ident_bf16[:])
+        ones_f32 = keep.tile([P, P], F32)
+        nc.vector.memset(ones_f32[:], 1.0)
+        table_in = keep.tile([P, 1], F32)
+        nc.vector.memset(table_in[:], 1.0)
+        table_out = keep.tile([P, 3], F32)
+
+        cl_sb = keep.tile([P, PACK, K], BF16)
+        for u in range(2):
+            nc.scalar.dma_start(
+                out=cl_sb[:, 2 * u : 2 * u + 2, :],
+                in_=clusters[256 * u : 256 * u + 256, :].rearrange("(q e) k -> q e k", e=2),
+            )
+        c2_sb = keep.tile([P, D_BLOCKS, K], BF16)
+        nc.scalar.dma_start(out=c2_sb[:], in_=clusters2[0].rearrange("(t p) k -> p t k", p=P))
+        gb_rows = keep.tile([P, P], BF16)
+        nc.vector.memset(gb_rows[:], 0.0)
+        nc.scalar.dma_start(out=gb_rows[0:1, :], in_=bn_gamma.rearrange("(o k) -> o k", o=1))
+        nc.scalar.dma_start(out=gb_rows[1:2, :], in_=bn_beta.rearrange("(o k) -> o k", o=1))
+        nc.scalar.sqrt(table_out[:, 0:1], table_in[:])
+
+        cl_grouped = keep.tile([P, K, PACK], BF16, align_bytes=64)
+        nc.vector.tensor_copy(out=cl_grouped[:], in_=cl_sb[:].rearrange("q t k -> q k t"))
+        cl_codes = keep.tile([P, K], U32, align_bytes=64)
+        cl_scales = keep.tile([P, K], U8, align_bytes=64)
+        nc.vector.quantize_mx(
+            out=cl_codes[:].bitcast(FP8X4),
+            scales=cl_scales[:],
+            in_=cl_grouped[:].rearrange("q k t -> q (k t)"),
+        )
+
+        c2T = keep.tile([P, D], F32)
+        gb = keep.tile([P, 2], F32)
+
+        xd_codes = keep.tile([P, CHUNKS, K_PASS], U32, align_bytes=64)
+        xd_scales = keep.tile([P, CHUNKS, K_PASS], U8, align_bytes=64)
+        xn_codes = keep.tile([P, CHUNKS, D], U32, align_bytes=64)
+        xn_scales = keep.tile([P, CHUNKS, D], U8, align_bytes=64)
+        stats = keep.tile([P, CHUNKS, 6], F32)
+        aT = {}
+
+        def project(psum, c):
+            aT[c] = psum.tile([P, K_PASS], F32, name="aT")
+            nc.tensor.matmul_mx(
+                out=aT[c][:],
+                lhsT=cl_codes[:].bitcast(FP8X4),
+                lhsT_scale=cl_scales[:],
+                rhs=xd_codes[:, c, :].bitcast(FP8X4),
+                rhs_scale=xd_scales[:, c, :],
+                start=True,
+                stop=True,
+            )
+
+        with ExitStack() as ph1:
+            xin = ph1.enter_context(tc.tile_pool(name="xin", bufs=LOAD_AHEAD + 2))
+            grp = ph1.enter_context(tc.tile_pool(name="grp", bufs=3))
+            ps_set = ph1.enter_context(tc.psum_pool(name="ps_set", bufs=1))
+            ps_xt = ph1.enter_context(tc.psum_pool(name="ps_xt", bufs=4))
+            ps_a1 = ph1.enter_context(tc.psum_pool(name="ps_a1", bufs=2))
+            x_sb, xt, gd, gn = {}, {}, {}, {}
+
+            def transpose_small_inputs():
+                c2T_ps = ps_set.tile([P, D_BLOCKS, P], BF16)
+                for t in range(D_BLOCKS):
+                    nc.tensor.transpose(c2T_ps[:, t, :], c2_sb[:, t, :], ident_bf16[:])
+                nc.vector.tensor_copy(out=c2T[:], in_=c2T_ps[:].rearrange("k t p -> k (t p)"))
+                gb_ps = ps_set.tile([P, P], BF16)
+                nc.tensor.transpose(gb_ps[:], gb_rows[:], ident_bf16[:])
+                nc.vector.tensor_copy(out=gb[:], in_=gb_ps[:, 0:2])
+
+            def load(c):
+                x_sb[c] = xin.tile([P, PACK, D], BF16, name="x_sb")
+                nc.sync.dma_start(
+                    out=x_sb[c][:],
+                    in_=x_rows[c * K_PASS : (c + 1) * K_PASS, :].rearrange("(p j) d -> p j d", j=PACK),
+                )
+
+            def transpose_words(c):
+                x_words = x_sb[c][:].bitcast(F32)
+                xt[c] = []
+                for h in range(2):
+                    bank = ps_xt.tile([P, 2, 2 * P], F32, name="xt")
+                    for u in range(2):
+                        for jj in range(2):
+                            nc.tensor.transpose(
+                                bank[:, u, jj * P : (jj + 1) * P],
+                                x_words[:, 2 * h + jj, u * P : (u + 1) * P],
+                                ident_f32[:],
+                            )
+                    xt[c].append(bank)
+
+            def copy_words(c):
+                gd[c] = grp.tile([P, K_PASS, PACK], BF16, align_bytes=64, name="gd")
+                gd_words = gd[c][:].bitcast(F32)
+                for h in range(2):
+                    nc.scalar.copy(
+                        out=gd_words[:, h * 2 * P : (h + 1) * 2 * P, :],
+                        in_=xt[c][h][:].rearrange("q u n -> q n u"),
+                    )
+
+            def quantise_along_d(c):
+                nc.vector.quantize_mx(
+                    out=xd_codes[:, c, :].bitcast(FP8X4),
+                    scales=xd_scales[:, c, :],
+                    in_=gd[c][:].rearrange("q n t -> q (n t)"),
+                )
+
+            def regroup(c):
+                gn[c] = grp.tile([P, D, PACK], BF16, align_bytes=64, name="gn")
+                dst = gn[c][:].rearrange("p (c i) j -> p c j i", i=4)
+                src = x_sb[c][:].rearrange("p j (c i) -> p c j i", i=4)
+                cut = SCALAR_D // 4
+                nc.scalar.copy(out=dst[:, 0:cut], in_=src[:, 0:cut])
+                nc.vector.tensor_copy(out=dst[:, cut:], in_=src[:, cut:])
+
+            def quantise_along_n(c):
+                nc.vector.quantize_mx(
+                    out=xn_codes[:, c, :].bitcast(FP8X4),
+                    scales=xn_scales[:, c, :],
+                    in_=gn[c][:].rearrange("p d j -> p (d j)"),
+                )
+
+            for s in range(-LOAD_AHEAD, CHUNKS + 1):
+                if live(s + LOAD_AHEAD):
+                    load(s + LOAD_AHEAD)
+                if live(s + 1):
+                    transpose_words(s + 1)
+                if s == SETUP_STEP:
+                    transpose_small_inputs()
+                if live(s - 1):
+                    quantise_along_d(s - 1)
+                    project(ps_a1, s - 1)
+                if live(s):
+                    copy_words(s)
+                    regroup(s)
+                if live(s - 1):
+                    quantise_along_n(s - 1)
+                    nc.vector.bn_stats(out=stats[:, s - 1, :], in_=aT[s - 1][:])
+
+        mean_var = keep.tile([P, 2], F32)
+        nc.vector.bn_aggr(out=mean_var[:], in_=stats[:].rearrange("p c s -> p (c s)"))
+        rstd = keep.tile([P, 1], F32)
+        nc.vector.tensor_scalar_add(out=rstd[:], in0=mean_var[:, 1:2], scalar1=BN_EPS)
+        nc.scalar.sqrt(rstd[:], rstd[:])
+        nc.scalar.activation(out=table_out[:, 1:2], in_=table_in[:], func=ACT.Exp)
+        nc.vector.reciprocal(rstd[:], rstd[:])
+        bn_scale = keep.tile([P, 1], F32)
+        nc.vector.tensor_mul(out=bn_scale[:], in0=gb[:, 0:1], in1=rstd[:])
+        bn_shift = keep.tile([P, 1], F32)
+        nc.vector.tensor_mul(out=bn_shift[:], in0=mean_var[:, 0:1], in1=bn_scale[:])
+        nc.vector.tensor_sub(out=bn_shift[:], in0=gb[:, 1:2], in1=bn_shift[:])
+
+        v_all = keep.tile([P, B, D], F32)
+        neg_asum = keep.tile([P, B], F32)
+        sumsq = keep.tile([P, B], F32)
+
+        with ExitStack() as ph2:
+            work = ph2.enter_context(tc.tile_pool(name="work", bufs=3))
+            ps_a2 = ph2.enter_context(tc.psum_pool(name="ps_a2", bufs=2))
+            ps_z = ph2.enter_context(tc.psum_pool(name="ps_z", bufs=3))
+            ps_v = ph2.enter_context(tc.psum_pool(name="ps_v", bufs=2))
+            ps_s = ph2.enter_context(tc.psum_pool(name="ps_s", bufs=1))
+            zT, z, neg_max, e, row_sum, inv_sum, pg, p_codes, p_scales, vT = {}, {}, {}, {}, {}, {}, {}, {}, {}, {}
+            asum = ps_s.tile([P, B], F32)
+
+            def normalise(c):
+                zT[c] = work.tile([P, K_PASS], F32, name="zT")
+                nc.scalar.activation(
+                    out=zT[c][:], in_=aT[c][:], func=ACT.Identity, scale=bn_scale[:, 0:1], bias=bn_shift[:, 0:1]
+                )
+
+            def to_rows(c):
+                z[c] = ps_z.tile([P, PACK, K], F32, name="z")
+                for j in range(PACK):
+                    nc.tensor.transpose(z[c][:, j, :], zT[c][:, j * P : (j + 1) * P], ident_f32[:])
+
+            def row_max(c):
+                neg_max[c] = work.tile([P, PACK], F32, name="neg_max")
+                nc.vector.tensor_reduce(out=neg_max[c][:], in_=z[c][:], axis=AX.X, op=ALU.max, negate=True)
+
+            def exponentials(c):
+                e[c] = work.tile([P, PACK, K], F32, name="e")
+                row_sum[c] = work.tile([P, PACK], F32, name="row_sum")
+                for j in range(PACK):
+                    nc.scalar.activation(
+                        out=e[c][:, j, :],
+                        in_=z[c][:, j, :],
+                        func=ACT.Exp,
+                        bias=neg_max[c][:, j : j + 1],
+                        scale=1.0,
+                        accum_out=row_sum[c][:, j : j + 1],
+                    )
+
+            def probabilities(c):
+                inv_sum[c] = work.tile([P, PACK], F32, name="inv_sum")
+                nc.vector.reciprocal(inv_sum[c][:], row_sum[c][:])
+                pg[c] = work.tile([P, K, PACK], BF16, align_bytes=64, name="pg")
+                nc.vector.tensor_tensor(
+                    out=pg[c][:],
+                    in0=e[c][:].rearrange("p j k -> p k j"),
+                    in1=inv_sum[c][:].unsqueeze(1).to_broadcast([P, K, PACK]),
+                    op=ALU.mult,
+                )
+
+            def sum_of_p(c):
+                b, cc = divmod(c, CHUNKS_PER_BATCH)
+                for j in range(PACK):
+                    nc.tensor.matmul(
+                        out=asum[:, b : b + 1],
+                        lhsT=e[c][:, j, :],
+                        rhs=inv_sum[c][:, j : j + 1],
+                        start=(cc == 0 and j == 0),
+                        stop=(cc == CHUNKS_PER_BATCH - 1 and j == PACK - 1),
+                    )
+
+            def quantise_p(c):
+                p_codes[c] = work.tile([P, K], U32, align_bytes=64, name="p_codes")
+                p_scales[c] = work.tile([P, K], U8, align_bytes=64, name="p_scales")
+                nc.vector.quantize_mx(
+                    out=p_codes[c][:].bitcast(FP8X4),
+                    scales=p_scales[c][:],
+                    in_=pg[c][:].rearrange("p k j -> p (k j)"),
+                )
+
+            def pool_chunk(c):
+                b, cc = divmod(c, CHUNKS_PER_BATCH)
+                if cc == 0:
+                    vT[b] = ps_v.tile([P, D], F32, name="vT")
+                nc.tensor.matmul_mx(
+                    out=vT[b][:],
+                    lhsT=p_codes[c][:].bitcast(FP8X4),
+                    lhsT_scale=p_scales[c][:],
+                    rhs=xn_codes[:, c, :].bitcast(FP8X4),
+                    rhs_scale=xn_scales[:, c, :],
+                    start=(cc == 0),
+                    stop=(cc == CHUNKS_PER_BATCH - 1),
+                )
+
+            def subtract_centres(b):
+                nc.vector.tensor_scalar_mul(out=neg_asum[:, b : b + 1], in0=asum[:, b : b + 1], scalar1=-1.0)
+                nc.vector.scalar_tensor_tensor(
+                    out=v_all[:, b, :],
+                    in0=c2T[:],
+                    scalar=neg_asum[:, b : b + 1],
+                    in1=vT[b][:],
+                    op0=ALU.mult,
+                    op1=ALU.add,
+                )
+
+            def sum_of_squares(b):
+                squares = work.tile([P, D], F32, name="squares")
+                nc.scalar.activation(
+                    out=squares[:], in_=v_all[:, b, :], func=ACT.Square, accum_out=sumsq[:, b : b + 1]
+                )
+
+            for s in range(-3, CHUNKS + 3):
+                batch_done = live(s - 3) and (s - 3) % CHUNKS_PER_BATCH == CHUNKS_PER_BATCH - 1
+                if live(s - 3):
+                    pool_chunk(s - 3)
+                if live(s + 3):
+                    project(ps_a2, s + 3)
+                if live(s + 2):
+                    normalise(s + 2)
+                    to_rows(s + 2)
+                if live(s - 2):
+                    sum_of_p(s - 2)
+                if live(s + 1):
+                    row_max(s + 1)
+                if batch_done:
+                    subtract_centres((s - 3) // CHUNKS_PER_BATCH)
+                if live(s):
+                    exponentials(s)
+                if s == CHUNKS:
+                    nc.scalar.sqrt(table_out[:, 2:3], table_in[:])
+                if batch_done:
+                    sum_of_squares((s - 3) // CHUNKS_PER_BATCH)
+                if live(s - 1):
+                    probabilities(s - 1)
+                    quantise_p(s - 1)
+
+        with ExitStack() as ph3:
+            fin = ph3.enter_context(tc.tile_pool(name="fin", bufs=3))
+            ps_t = ph3.enter_context(tc.psum_pool(name="ps_t", bufs=1))
+            ps_o = ph3.enter_context(tc.psum_pool(name="ps_o", bufs=3))
+            inv1 = keep.tile([P, B], F32)
+            nc.scalar.sqrt(inv1[:], sumsq[:])
+            nc.vector.tensor_scalar_max(out=inv1[:], in0=inv1[:], scalar1=NORM_EPS)
+            nc.vector.reciprocal(inv1[:], inv1[:])
+            part = keep.tile([P, B], F32)
+            nc.vector.tensor_mul(out=part[:], in0=sumsq[:], in1=inv1[:])
+            nc.vector.tensor_mul(out=part[:], in0=part[:], in1=inv1[:])
+            total = ps_t.tile([P, B], F32)
+            nc.tensor.matmul(out=total[:], lhsT=ones_f32[:], rhs=part[:], start=True, stop=True)
+            factor = keep.tile([P, B], F32)
+            nc.scalar.sqrt(factor[:], total[:])
+            nc.vector.tensor_scalar_max(out=factor[:], in0=factor[:], scalar1=NORM_EPS)
+            nc.vector.reciprocal(factor[:], factor[:])
+            nc.vector.tensor_mul(out=factor[:], in0=factor[:], in1=inv1[:])
+            oT = {}
+            for b in range(B + 1):
+                if b < B:
+                    scaled = fin.tile([P, D], F32, name="scaled")
+                    nc.vector.tensor_scalar_mul(out=scaled[:], in0=v_all[:, b, :], scalar1=factor[:, b : b + 1])
+                    oT[b] = ps_o.tile([P, D_BLOCKS, K], F32, name="oT")
+                    for t in range(D_BLOCKS):
+                        nc.tensor.transpose(oT[b][:, t, :], scaled[:, t * P : (t + 1) * P], ident_f32[:])
+                if b >= 1:
+                    o_sb = fin.tile([P, D_BLOCKS, K], F32, name="o_sb")
+                    nc.scalar.copy(out=o_sb[:], in_=oT[b - 1][:])
+                    nc.sync.dma_start(
+                        out=out[b - 1].rearrange("(t p k) -> p t k", t=D_BLOCKS, p=P), in_=o_sb[:]
+                    )

@@ -24,6 +24,7 @@ BN_EPS = 1e-5
 NORM_EPS = 1e-12
 SCALAR_D = 256
 LOAD_AHEAD = 4
+SUM_COLS = 32
 SETUP_STEP = 2
 
 FLOPS = 2 * 2 * ROWS * D * K
@@ -202,12 +203,13 @@ def tile_modelnew_kernel(tc, x, clusters, clusters2, bn_gamma, bn_beta, out):
 
         with ExitStack() as ph2:
             work = ph2.enter_context(tc.tile_pool(name="work", bufs=3))
+            rows = ph2.enter_context(tc.tile_pool(name="rows", bufs=4))
             ps_a2 = ph2.enter_context(tc.psum_pool(name="ps_a2", bufs=2))
             ps_z = ph2.enter_context(tc.psum_pool(name="ps_z", bufs=3))
             ps_v = ph2.enter_context(tc.psum_pool(name="ps_v", bufs=2))
             ps_s = ph2.enter_context(tc.psum_pool(name="ps_s", bufs=1))
             zT, z, neg_max, e, row_sum, inv_sum, pg, p_codes, p_scales, vT = {}, {}, {}, {}, {}, {}, {}, {}, {}, {}
-            asum = ps_s.tile([P, B], F32)
+            asum = ps_s.tile([P, B, SUM_COLS], F32)
 
             def normalise(c):
                 zT[c] = work.tile([P, K_PASS], F32, name="zT")
@@ -225,8 +227,8 @@ def tile_modelnew_kernel(tc, x, clusters, clusters2, bn_gamma, bn_beta, out):
                 nc.vector.tensor_reduce(out=neg_max[c][:], in_=z[c][:], axis=AX.X, op=ALU.max, negate=True)
 
             def exponentials(c):
-                e[c] = work.tile([P, PACK, K], F32, name="e")
-                row_sum[c] = work.tile([P, PACK], F32, name="row_sum")
+                e[c] = rows.tile([P, PACK, K], F32, name="e")
+                row_sum[c] = rows.tile([P, PACK], F32, name="row_sum")
                 for j in range(PACK):
                     nc.scalar.activation(
                         out=e[c][:, j, :],
@@ -237,9 +239,11 @@ def tile_modelnew_kernel(tc, x, clusters, clusters2, bn_gamma, bn_beta, out):
                         accum_out=row_sum[c][:, j : j + 1],
                     )
 
-            def probabilities(c):
-                inv_sum[c] = work.tile([P, PACK], F32, name="inv_sum")
+            def invert_sums(c):
+                inv_sum[c] = rows.tile([P, PACK], F32, name="inv_sum")
                 nc.vector.reciprocal(inv_sum[c][:], row_sum[c][:])
+
+            def probabilities(c):
                 pg[c] = work.tile([P, K, PACK], BF16, align_bytes=64, name="pg")
                 nc.vector.tensor_tensor(
                     out=pg[c][:],
@@ -252,9 +256,9 @@ def tile_modelnew_kernel(tc, x, clusters, clusters2, bn_gamma, bn_beta, out):
                 b, cc = divmod(c, CHUNKS_PER_BATCH)
                 for j in range(PACK):
                     nc.tensor.matmul(
-                        out=asum[:, b : b + 1],
+                        out=asum[:, b, :],
                         lhsT=e[c][:, j, :],
-                        rhs=inv_sum[c][:, j : j + 1],
+                        rhs=inv_sum[c][:, j : j + 1].to_broadcast([P, SUM_COLS]),
                         start=(cc == 0 and j == 0),
                         stop=(cc == CHUNKS_PER_BATCH - 1 and j == PACK - 1),
                     )
@@ -283,7 +287,7 @@ def tile_modelnew_kernel(tc, x, clusters, clusters2, bn_gamma, bn_beta, out):
                 )
 
             def subtract_centres(b):
-                nc.vector.tensor_scalar_mul(out=neg_asum[:, b : b + 1], in0=asum[:, b : b + 1], scalar1=-1.0)
+                nc.vector.tensor_scalar_mul(out=neg_asum[:, b : b + 1], in0=asum[:, b, 0:1], scalar1=-1.0)
                 nc.vector.scalar_tensor_tensor(
                     out=v_all[:, b, :],
                     in0=c2T[:],
@@ -299,30 +303,34 @@ def tile_modelnew_kernel(tc, x, clusters, clusters2, bn_gamma, bn_beta, out):
                     out=squares[:], in_=v_all[:, b, :], func=ACT.Square, accum_out=sumsq[:, b : b + 1]
                 )
 
-            for s in range(-3, CHUNKS + 3):
+            for s in range(-4, CHUNKS + 3):
                 batch_done = live(s - 3) and (s - 3) % CHUNKS_PER_BATCH == CHUNKS_PER_BATCH - 1
                 if live(s - 3):
                     pool_chunk(s - 3)
-                if live(s + 3):
-                    project(ps_a2, s + 3)
+                if live(s + 4):
+                    project(ps_a2, s + 4)
                 if live(s + 2):
-                    normalise(s + 2)
                     to_rows(s + 2)
+                if live(s + 3):
+                    normalise(s + 3)
                 if live(s - 2):
                     sum_of_p(s - 2)
+                if live(s - 1):
+                    invert_sums(s - 1)
                 if live(s + 1):
                     row_max(s + 1)
+                if live(s - 1):
+                    probabilities(s - 1)
                 if batch_done:
                     subtract_centres((s - 3) // CHUNKS_PER_BATCH)
+                if live(s - 2):
+                    quantise_p(s - 2)
                 if live(s):
                     exponentials(s)
                 if s == CHUNKS:
                     nc.scalar.sqrt(table_out[:, 2:3], table_in[:])
                 if batch_done:
                     sum_of_squares((s - 3) // CHUNKS_PER_BATCH)
-                if live(s - 1):
-                    probabilities(s - 1)
-                    quantise_p(s - 1)
 
         with ExitStack() as ph3:
             fin = ph3.enter_context(tc.tile_pool(name="fin", bufs=3))

@@ -24,7 +24,6 @@ BN_EPS = 1e-5
 NORM_EPS = 1e-12
 SCALAR_D = 256
 LOAD_AHEAD = 4
-SUM_COLS = 32
 SETUP_STEP = 2
 
 FLOPS = 2 * 2 * ROWS * D * K
@@ -208,8 +207,8 @@ def tile_modelnew_kernel(tc, x, clusters, clusters2, bn_gamma, bn_beta, out):
             ps_z = ph2.enter_context(tc.psum_pool(name="ps_z", bufs=3))
             ps_v = ph2.enter_context(tc.psum_pool(name="ps_v", bufs=2))
             ps_s = ph2.enter_context(tc.psum_pool(name="ps_s", bufs=1))
-            zT, z, neg_max, e, row_sum, inv_sum, pg, p_codes, p_scales, vT = {}, {}, {}, {}, {}, {}, {}, {}, {}, {}
-            asum = ps_s.tile([P, B, SUM_COLS], F32)
+            zT, z, neg_max, e, row_sum, inv_sum, pf, pg, p_codes, p_scales, vT = {}, {}, {}, {}, {}, {}, {}, {}, {}, {}, {}
+            p_sums = ps_s.tile([P, 4, P], F32)
 
             def normalise(c):
                 zT[c] = work.tile([P, K_PASS], F32, name="zT")
@@ -244,21 +243,26 @@ def tile_modelnew_kernel(tc, x, clusters, clusters2, bn_gamma, bn_beta, out):
                 nc.vector.reciprocal(inv_sum[c][:], row_sum[c][:])
 
             def probabilities(c):
-                pg[c] = work.tile([P, K, PACK], BF16, align_bytes=64, name="pg")
+                pf[c] = work.tile([P, PACK, K], F32, name="pf")
                 nc.vector.tensor_tensor(
-                    out=pg[c][:],
-                    in0=e[c][:].rearrange("p j k -> p k j"),
-                    in1=inv_sum[c][:].unsqueeze(1).to_broadcast([P, K, PACK]),
+                    out=pf[c][:],
+                    in0=e[c][:],
+                    in1=inv_sum[c][:].unsqueeze(2).to_broadcast([P, PACK, K]),
                     op=ALU.mult,
                 )
+
+            def round_p(c):
+                pg[c] = work.tile([P, K, PACK], BF16, align_bytes=64, name="pg")
+                nc.vector.tensor_copy(out=pg[c][:], in_=pf[c][:].rearrange("p j k -> p k j"))
 
             def sum_of_p(c):
                 b, cc = divmod(c, CHUNKS_PER_BATCH)
                 for j in range(PACK):
                     nc.tensor.matmul(
-                        out=asum[:, b, :],
-                        lhsT=e[c][:, j, :],
-                        rhs=inv_sum[c][:, j : j + 1].to_broadcast([P, SUM_COLS]),
+                        out=p_sums[:, b % 4, :],
+                        lhsT=pf[c][:, j, :],
+                        rhs=ident_f32[:],
+                        is_transpose=True,
                         start=(cc == 0 and j == 0),
                         stop=(cc == CHUNKS_PER_BATCH - 1 and j == PACK - 1),
                     )
@@ -287,7 +291,9 @@ def tile_modelnew_kernel(tc, x, clusters, clusters2, bn_gamma, bn_beta, out):
                 )
 
             def subtract_centres(b):
-                nc.vector.tensor_scalar_mul(out=neg_asum[:, b : b + 1], in0=asum[:, b, 0:1], scalar1=-1.0)
+                nc.vector.tensor_reduce(
+                    out=neg_asum[:, b : b + 1], in_=p_sums[:, b % 4, :], axis=AX.X, op=ALU.add, negate=True
+                )
                 nc.vector.scalar_tensor_tensor(
                     out=v_all[:, b, :],
                     in0=c2T[:],
@@ -325,6 +331,8 @@ def tile_modelnew_kernel(tc, x, clusters, clusters2, bn_gamma, bn_beta, out):
                     subtract_centres((s - 3) // CHUNKS_PER_BATCH)
                 if live(s - 2):
                     quantise_p(s - 2)
+                if live(s - 1):
+                    round_p(s - 1)
                 if live(s):
                     exponentials(s)
                 if s == CHUNKS:

@@ -22,7 +22,10 @@ CHUNKS_PER_BATCH = N // K_PASS
 D_BLOCKS = D // P
 BN_EPS = 1e-5
 NORM_EPS = 1e-12
-SCALAR_D = 256
+D_LATE = 128
+D_EARLY = D - D_LATE
+D_CALL = 256
+SCALAR_D = 208
 LOAD_AHEAD = 4
 SETUP_STEP = 2
 
@@ -152,19 +155,20 @@ def tile_modelnew_kernel(tc, x, clusters, clusters2, bn_gamma, bn_beta, out):
                 )
 
             def regroup(c):
-                gn[c] = grp.tile([P, D, PACK], BF16, align_bytes=64, name="gn")
+                gn[c] = grp.tile([P, D_EARLY, PACK], BF16, align_bytes=64, name="gn")
                 dst = gn[c][:].rearrange("p (c i) j -> p c j i", i=4)
-                src = x_sb[c][:].rearrange("p j (c i) -> p c j i", i=4)
+                src = x_sb[c][:, :, 0:D_EARLY].rearrange("p j (c i) -> p c j i", i=4)
                 cut = SCALAR_D // 4
                 nc.scalar.copy(out=dst[:, 0:cut], in_=src[:, 0:cut])
                 nc.vector.tensor_copy(out=dst[:, cut:], in_=src[:, cut:])
 
             def quantise_along_n(c):
-                nc.vector.quantize_mx(
-                    out=xn_codes[:, c, :].bitcast(FP8X4),
-                    scales=xn_scales[:, c, :],
-                    in_=gn[c][:].rearrange("p d j -> p (d j)"),
-                )
+                for cols in (slice(0, D_CALL), slice(D_CALL, D_EARLY)):
+                    nc.vector.quantize_mx(
+                        out=xn_codes[:, c, cols].bitcast(FP8X4),
+                        scales=xn_scales[:, c, cols],
+                        in_=gn[c][:, cols, :].rearrange("p d j -> p (d j)"),
+                    )
 
             for s in range(-LOAD_AHEAD, CHUNKS + 1):
                 if live(s + LOAD_AHEAD):
@@ -203,12 +207,35 @@ def tile_modelnew_kernel(tc, x, clusters, clusters2, bn_gamma, bn_beta, out):
         with ExitStack() as ph2:
             work = ph2.enter_context(tc.tile_pool(name="work", bufs=3))
             rows = ph2.enter_context(tc.tile_pool(name="rows", bufs=4))
+            late = ph2.enter_context(tc.tile_pool(name="late", bufs=LOAD_AHEAD + 2))
+            x_late, g_late = {}, {}
             ps_a2 = ph2.enter_context(tc.psum_pool(name="ps_a2", bufs=2))
             ps_z = ph2.enter_context(tc.psum_pool(name="ps_z", bufs=3))
             ps_v = ph2.enter_context(tc.psum_pool(name="ps_v", bufs=2))
             ps_s = ph2.enter_context(tc.psum_pool(name="ps_s", bufs=1))
             zT, z, neg_max, e, row_sum, inv_sum, pf, pg, p_codes, p_scales, vT = {}, {}, {}, {}, {}, {}, {}, {}, {}, {}, {}
             p_sums = ps_s.tile([P, 4, P], F32)
+
+            def load_late(c):
+                x_late[c] = late.tile([P, PACK, D_LATE], BF16, name="x_late")
+                nc.sync.dma_start(
+                    out=x_late[c][:],
+                    in_=x_rows[c * K_PASS : (c + 1) * K_PASS, D_EARLY:D].rearrange("(p j) d -> p j d", j=PACK),
+                )
+
+            def regroup_late(c):
+                g_late[c] = late.tile([P, D_LATE, PACK], BF16, align_bytes=64, name="g_late")
+                nc.scalar.copy(
+                    out=g_late[c][:].rearrange("p (c i) j -> p c j i", i=4),
+                    in_=x_late[c][:].rearrange("p j (c i) -> p c j i", i=4),
+                )
+
+            def quantise_late(c):
+                nc.vector.quantize_mx(
+                    out=xn_codes[:, c, D_EARLY:D].bitcast(FP8X4),
+                    scales=xn_scales[:, c, D_EARLY:D],
+                    in_=g_late[c][:].rearrange("p d j -> p (d j)"),
+                )
 
             def normalise(c):
                 zT[c] = work.tile([P, K_PASS], F32, name="zT")
@@ -309,7 +336,9 @@ def tile_modelnew_kernel(tc, x, clusters, clusters2, bn_gamma, bn_beta, out):
                     out=squares[:], in_=v_all[:, b, :], func=ACT.Square, accum_out=sumsq[:, b : b + 1]
                 )
 
-            for s in range(-4, CHUNKS + 3):
+            for s in range(-LOAD_AHEAD, CHUNKS + 3):
+                if live(s + LOAD_AHEAD):
+                    load_late(s + LOAD_AHEAD)
                 batch_done = live(s - 3) and (s - 3) % CHUNKS_PER_BATCH == CHUNKS_PER_BATCH - 1
                 if live(s - 3):
                     pool_chunk(s - 3)
@@ -333,8 +362,10 @@ def tile_modelnew_kernel(tc, x, clusters, clusters2, bn_gamma, bn_beta, out):
                     quantise_p(s - 2)
                 if live(s - 1):
                     round_p(s - 1)
+                    quantise_late(s - 1)
                 if live(s):
                     exponentials(s)
+                    regroup_late(s)
                 if s == CHUNKS:
                     nc.scalar.sqrt(table_out[:, 2:3], table_in[:])
                 if batch_done:

@@ -170,7 +170,7 @@ def tile_modelnew_kernel(tc, x, clusters, clusters2, bn_gamma, bn_beta, out):
                         in_=gn[c][:, cols, :].rearrange("p d j -> p (d j)"),
                     )
 
-            for s in range(-LOAD_AHEAD, CHUNKS + 1):
+            for s in range(-LOAD_AHEAD, CHUNKS + 2):
                 if live(s + LOAD_AHEAD):
                     load(s + LOAD_AHEAD)
                 if live(s + 1):
@@ -185,7 +185,8 @@ def tile_modelnew_kernel(tc, x, clusters, clusters2, bn_gamma, bn_beta, out):
                     regroup(s)
                 if live(s - 1):
                     quantise_along_n(s - 1)
-                    nc.vector.bn_stats(out=stats[:, s - 1, :], in_=aT[s - 1][:])
+                if live(s - 2):
+                    nc.vector.bn_stats(out=stats[:, s - 2, :], in_=aT[s - 2][:])
 
         mean_var = keep.tile([P, 2], F32)
         nc.vector.bn_aggr(out=mean_var[:], in_=stats[:].rearrange("p c s -> p (c s)"))

@@ -25,6 +25,7 @@ NORM_EPS = 1e-12
 D_LATE = 128
 D_EARLY = D - D_LATE
 D_CALL = 256
+SCALAR_LATE = 64
 SCALAR_D = 208
 LOAD_AHEAD = 4
 SETUP_STEP = 2
@@ -52,7 +53,7 @@ def tile_modelnew_kernel(tc, x, clusters, clusters2, bn_gamma, bn_beta, out):
         nc.vector.memset(ones_f32[:], 1.0)
         table_in = keep.tile([P, 1], F32)
         nc.vector.memset(table_in[:], 1.0)
-        table_out = keep.tile([P, 3], F32)
+        table_out = keep.tile([P, 2], F32)
 
         cl_sb = keep.tile([P, PACK, K], BF16)
         for u in range(2):
@@ -66,7 +67,7 @@ def tile_modelnew_kernel(tc, x, clusters, clusters2, bn_gamma, bn_beta, out):
         nc.vector.memset(gb_rows[:], 0.0)
         nc.scalar.dma_start(out=gb_rows[0:1, :], in_=bn_gamma.rearrange("(o k) -> o k", o=1))
         nc.scalar.dma_start(out=gb_rows[1:2, :], in_=bn_beta.rearrange("(o k) -> o k", o=1))
-        nc.scalar.sqrt(table_out[:, 0:1], table_in[:])
+        nc.scalar.activation(out=table_out[:, 0:1], in_=table_in[:], func=ACT.Exp)
 
         cl_grouped = keep.tile([P, K, PACK], BF16, align_bytes=64)
         nc.vector.tensor_copy(out=cl_grouped[:], in_=cl_sb[:].rearrange("q t k -> q k t"))
@@ -190,30 +191,33 @@ def tile_modelnew_kernel(tc, x, clusters, clusters2, bn_gamma, bn_beta, out):
 
         mean_var = keep.tile([P, 2], F32)
         nc.vector.bn_aggr(out=mean_var[:], in_=stats[:].rearrange("p c s -> p (c s)"))
+        neg_half = keep.tile([P, 1], F32)
+        nc.gpsimd.memset(neg_half[:], -0.5)
+        var_eps = keep.tile([P, 1], F32)
+        nc.vector.tensor_scalar_add(out=var_eps[:], in0=mean_var[:, 1:2], scalar1=BN_EPS)
+        neg_mean = keep.tile([P, 1], F32)
+        nc.vector.tensor_scalar_mul(out=neg_mean[:], in0=mean_var[:, 0:1], scalar1=-1.0)
         rstd = keep.tile([P, 1], F32)
-        nc.vector.tensor_scalar_add(out=rstd[:], in0=mean_var[:, 1:2], scalar1=BN_EPS)
-        nc.scalar.sqrt(rstd[:], rstd[:])
-        nc.scalar.activation(out=table_out[:, 1:2], in_=table_in[:], func=ACT.Exp)
-        nc.vector.reciprocal(rstd[:], rstd[:])
+        nc.gpsimd.tensor_tensor(out=rstd[:], in0=var_eps[:], in1=neg_half[:], op=ALU.pow)
         bn_scale = keep.tile([P, 1], F32)
         nc.vector.tensor_mul(out=bn_scale[:], in0=gb[:, 0:1], in1=rstd[:])
         bn_shift = keep.tile([P, 1], F32)
-        nc.vector.tensor_mul(out=bn_shift[:], in0=mean_var[:, 0:1], in1=bn_scale[:])
-        nc.vector.tensor_sub(out=bn_shift[:], in0=gb[:, 1:2], in1=bn_shift[:])
-
-        v_all = keep.tile([P, B, D], F32)
-        neg_asum = keep.tile([P, B], F32)
-        sumsq = keep.tile([P, B], F32)
+        nc.vector.scalar_tensor_tensor(
+            out=bn_shift[:], in0=neg_mean[:], scalar=bn_scale[:, 0:1], in1=gb[:, 1:2], op0=ALU.mult, op1=ALU.add
+        )
 
         with ExitStack() as ph2:
             work = ph2.enter_context(tc.tile_pool(name="work", bufs=3))
             rows = ph2.enter_context(tc.tile_pool(name="rows", bufs=4))
             late = ph2.enter_context(tc.tile_pool(name="late", bufs=LOAD_AHEAD + 2))
+            outs = ph2.enter_context(tc.tile_pool(name="outs", bufs=3))
+            norms = ph2.enter_context(tc.tile_pool(name="norms", bufs=3))
             x_late, g_late = {}, {}
             ps_a2 = ph2.enter_context(tc.psum_pool(name="ps_a2", bufs=2))
             ps_z = ph2.enter_context(tc.psum_pool(name="ps_z", bufs=3))
             ps_v = ph2.enter_context(tc.psum_pool(name="ps_v", bufs=2))
             ps_s = ph2.enter_context(tc.psum_pool(name="ps_s", bufs=1))
+            v, sumsq, inv1, total_sb, factor, scaled, oT = {}, {}, {}, {}, {}, {}, {}
             zT, z, neg_max, e, row_sum, inv_sum, pf, pg, p_codes, p_scales, vT = {}, {}, {}, {}, {}, {}, {}, {}, {}, {}, {}
             p_sums = ps_s.tile([P, 4, P], F32)
 
@@ -226,10 +230,13 @@ def tile_modelnew_kernel(tc, x, clusters, clusters2, bn_gamma, bn_beta, out):
 
             def regroup_late(c):
                 g_late[c] = late.tile([P, D_LATE, PACK], BF16, align_bytes=64, name="g_late")
-                nc.scalar.copy(
-                    out=g_late[c][:].rearrange("p (c i) j -> p c j i", i=4),
-                    in_=x_late[c][:].rearrange("p j (c i) -> p c j i", i=4),
-                )
+                dst = g_late[c][:].rearrange("p (c i) j -> p c j i", i=4)
+                late_src = x_late[c][:].rearrange("p j (c i) -> p c j i", i=4)
+                cut = SCALAR_LATE // 4
+                if cut > 0:
+                    nc.scalar.copy(out=dst[:, 0:cut], in_=late_src[:, 0:cut])
+                if cut < D_LATE // 4:
+                    nc.vector.tensor_copy(out=dst[:, cut:], in_=late_src[:, cut:])
 
             def quantise_late(c):
                 nc.vector.quantize_mx(
@@ -272,12 +279,10 @@ def tile_modelnew_kernel(tc, x, clusters, clusters2, bn_gamma, bn_beta, out):
 
             def probabilities(c):
                 pf[c] = work.tile([P, PACK, K], F32, name="pf")
-                nc.vector.tensor_tensor(
-                    out=pf[c][:],
-                    in0=e[c][:],
-                    in1=inv_sum[c][:].unsqueeze(2).to_broadcast([P, PACK, K]),
-                    op=ALU.mult,
-                )
+                for j in range(PACK):
+                    nc.vector.tensor_scalar_mul(
+                        out=pf[c][:, j, :], in0=e[c][:, j, :], scalar1=inv_sum[c][:, j : j + 1]
+                    )
 
             def round_p(c):
                 pg[c] = work.tile([P, K, PACK], BF16, align_bytes=64, name="pg")
@@ -319,34 +324,79 @@ def tile_modelnew_kernel(tc, x, clusters, clusters2, bn_gamma, bn_beta, out):
                 )
 
             def subtract_centres(b):
+                neg_asum = norms.tile([P, 1], F32, name="neg_asum")
                 nc.vector.tensor_reduce(
-                    out=neg_asum[:, b : b + 1], in_=p_sums[:, b % 4, :], axis=AX.X, op=ALU.add, negate=True
+                    out=neg_asum[:], in_=p_sums[:, b % 4, :], axis=AX.X, op=ALU.add, negate=True
                 )
+                v[b] = outs.tile([P, D], F32, name="v")
                 nc.vector.scalar_tensor_tensor(
-                    out=v_all[:, b, :],
-                    in0=c2T[:],
-                    scalar=neg_asum[:, b : b + 1],
-                    in1=vT[b][:],
-                    op0=ALU.mult,
-                    op1=ALU.add,
+                    out=v[b][:], in0=c2T[:], scalar=neg_asum[:, 0:1], in1=vT[b][:], op0=ALU.mult, op1=ALU.add
                 )
 
             def sum_of_squares(b):
-                squares = work.tile([P, D], F32, name="squares")
-                nc.scalar.activation(
-                    out=squares[:], in_=v_all[:, b, :], func=ACT.Square, accum_out=sumsq[:, b : b + 1]
-                )
+                squares = outs.tile([P, D], F32, name="squares")
+                sumsq[b] = norms.tile([P, 1], F32, name="sumsq")
+                nc.scalar.activation(out=squares[:], in_=v[b][:], func=ACT.Square, accum_out=sumsq[b][:, 0:1])
 
-            for s in range(-LOAD_AHEAD, CHUNKS + 3):
+            def rsqrt_floored(out_tile, x):
+                nc.gpsimd.tensor_tensor(out=out_tile[:], in0=x[:], in1=neg_half[:], op=ALU.pow)
+
+            def column_norms(b):
+                floored = norms.tile([P, 1], F32, name="floored")
+                nc.gpsimd.tensor_scalar(
+                    out=floored[:], in0=sumsq[b][:], scalar1=NORM_EPS * NORM_EPS, scalar2=None, op0=ALU.max
+                )
+                inv1[b] = norms.tile([P, 1], F32, name="inv1")
+                rsqrt_floored(inv1[b], floored)
+                part = norms.tile([P, 1], F32, name="part")
+                nc.gpsimd.tensor_tensor(out=part[:], in0=sumsq[b][:], in1=inv1[b][:], op=ALU.mult)
+                part2 = norms.tile([P, 1], F32, name="part2")
+                nc.gpsimd.tensor_tensor(out=part2[:], in0=part[:], in1=inv1[b][:], op=ALU.mult)
+                total_sb[b] = part2
+
+            def row_total(b):
+                nc.tensor.matmul(out=vT[b][:, 0:1], lhsT=ones_f32[:], rhs=total_sb[b][:], start=True, stop=True)
+
+            def row_norm(b):
+                total = norms.tile([P, 1], F32, name="total")
+                nc.vector.tensor_scalar_max(out=total[:], in0=vT[b][:, 0:1], scalar1=NORM_EPS * NORM_EPS)
+                inv2 = norms.tile([P, 1], F32, name="inv2")
+                rsqrt_floored(inv2, total)
+                factor[b] = norms.tile([P, 1], F32, name="factor")
+                nc.gpsimd.tensor_tensor(out=factor[b][:], in0=inv2[:], in1=inv1[b][:], op=ALU.mult)
+
+            def scale_rows(b):
+                scaled[b] = outs.tile([P, D], F32, name="scaled")
+                nc.vector.tensor_scalar_mul(out=scaled[b][:], in0=v[b][:], scalar1=factor[b][:, 0:1])
+
+            def to_out(b):
+                oT[b] = ps_z.tile([P, D_BLOCKS, K], F32, name="z")
+                for t in range(D_BLOCKS):
+                    nc.tensor.transpose(oT[b][:, t, :], scaled[b][:, t * P : (t + 1) * P], ident_f32[:])
+
+            def store(b):
+                o_sb = outs.tile([P, D_BLOCKS, K], F32, name="o_sb")
+                nc.scalar.copy(out=o_sb[:], in_=oT[b][:])
+                nc.sync.dma_start(out=out[b].rearrange("(t p k) -> p t k", t=D_BLOCKS, p=P), in_=o_sb[:])
+
+            def batch_at(s, lag):
+                c = s - 3 - lag
+                return c // CHUNKS_PER_BATCH if live(c) and c % CHUNKS_PER_BATCH == CHUNKS_PER_BATCH - 1 else None
+
+            for s in range(-LOAD_AHEAD, CHUNKS + 3 + 7):
                 if live(s + LOAD_AHEAD):
                     load_late(s + LOAD_AHEAD)
-                batch_done = live(s - 3) and (s - 3) % CHUNKS_PER_BATCH == CHUNKS_PER_BATCH - 1
+                done = [batch_at(s, lag) for lag in range(7)]
                 if live(s - 3):
                     pool_chunk(s - 3)
                 if live(s + 4):
                     project(ps_a2, s + 4)
+                if done[2] is not None:
+                    row_total(done[2])
                 if live(s + 2):
                     to_rows(s + 2)
+                if done[5] is not None:
+                    to_out(done[5])
                 if live(s + 3):
                     normalise(s + 3)
                 if live(s - 2):
@@ -357,50 +407,22 @@ def tile_modelnew_kernel(tc, x, clusters, clusters2, bn_gamma, bn_beta, out):
                     row_max(s + 1)
                 if live(s - 1):
                     probabilities(s - 1)
-                if batch_done:
-                    subtract_centres((s - 3) // CHUNKS_PER_BATCH)
+                if done[0] is not None:
+                    subtract_centres(done[0])
+                if done[3] is not None:
+                    row_norm(done[3])
+                if done[4] is not None:
+                    scale_rows(done[4])
                 if live(s - 2):
                     quantise_p(s - 2)
                 if live(s - 1):
                     round_p(s - 1)
                     quantise_late(s - 1)
+                if done[1] is not None:
+                    sum_of_squares(done[1])
+                    column_norms(done[1])
                 if live(s):
                     exponentials(s)
                     regroup_late(s)
-                if s == CHUNKS:
-                    nc.scalar.sqrt(table_out[:, 2:3], table_in[:])
-                if batch_done:
-                    sum_of_squares((s - 3) // CHUNKS_PER_BATCH)
-
-        with ExitStack() as ph3:
-            fin = ph3.enter_context(tc.tile_pool(name="fin", bufs=3))
-            ps_t = ph3.enter_context(tc.psum_pool(name="ps_t", bufs=1))
-            ps_o = ph3.enter_context(tc.psum_pool(name="ps_o", bufs=3))
-            inv1 = keep.tile([P, B], F32)
-            nc.scalar.sqrt(inv1[:], sumsq[:])
-            nc.vector.tensor_scalar_max(out=inv1[:], in0=inv1[:], scalar1=NORM_EPS)
-            nc.vector.reciprocal(inv1[:], inv1[:])
-            part = keep.tile([P, B], F32)
-            nc.vector.tensor_mul(out=part[:], in0=sumsq[:], in1=inv1[:])
-            nc.vector.tensor_mul(out=part[:], in0=part[:], in1=inv1[:])
-            total = ps_t.tile([P, B], F32)
-            nc.tensor.matmul(out=total[:], lhsT=ones_f32[:], rhs=part[:], start=True, stop=True)
-            factor = keep.tile([P, B], F32)
-            nc.scalar.sqrt(factor[:], total[:])
-            nc.vector.tensor_scalar_max(out=factor[:], in0=factor[:], scalar1=NORM_EPS)
-            nc.vector.reciprocal(factor[:], factor[:])
-            nc.vector.tensor_mul(out=factor[:], in0=factor[:], in1=inv1[:])
-            oT = {}
-            for b in range(B + 1):
-                if b < B:
-                    scaled = fin.tile([P, D], F32, name="scaled")
-                    nc.vector.tensor_scalar_mul(out=scaled[:], in0=v_all[:, b, :], scalar1=factor[:, b : b + 1])
-                    oT[b] = ps_o.tile([P, D_BLOCKS, K], F32, name="oT")
-                    for t in range(D_BLOCKS):
-                        nc.tensor.transpose(oT[b][:, t, :], scaled[:, t * P : (t + 1) * P], ident_f32[:])
-                if b >= 1:
-                    o_sb = fin.tile([P, D_BLOCKS, K], F32, name="o_sb")
-                    nc.scalar.copy(out=o_sb[:], in_=oT[b - 1][:])
-                    nc.sync.dma_start(
-                        out=out[b - 1].rearrange("(t p k) -> p t k", t=D_BLOCKS, p=P), in_=o_sb[:]
-                    )
+                if done[6] is not None:
+                    store(done[6])

@@ -25,10 +25,12 @@ NORM_EPS = 1e-12
 D_LATE = 128
 D_EARLY = D - D_LATE
 D_CALL = 256
-SCALAR_LATE = 64
 SCALAR_D = 208
+SCALAR_LATE = 96
 LOAD_AHEAD = 4
+LATE_FILL = 6
 SETUP_STEP = 2
+TAIL = 8
 
 FLOPS = 2 * 2 * ROWS * D * K
 
@@ -44,16 +46,21 @@ def tile_modelnew_kernel(tc, x, clusters, clusters2, bn_gamma, bn_beta, out):
     with ExitStack() as ctx:
         ctx.enter_context(tc.manual_schedule())
         keep = ctx.enter_context(tc.tile_pool(name="keep", bufs=1))
+        late = ctx.enter_context(tc.tile_pool(name="late", bufs=LATE_FILL + 4))
 
         ident_f32 = keep.tile([P, P], F32)
         make_identity(nc, ident_f32[:])
         ident_bf16 = keep.tile([P, P], BF16)
         make_identity(nc, ident_bf16[:])
-        ones_f32 = keep.tile([P, P], F32)
-        nc.vector.memset(ones_f32[:], 1.0)
         table_in = keep.tile([P, 1], F32)
         nc.vector.memset(table_in[:], 1.0)
-        table_out = keep.tile([P, 2], F32)
+        table_out = keep.tile([P, 1], F32)
+        neg_half = keep.tile([P, 2], F32)
+        nc.vector.memset(neg_half[:], -0.5)
+        eps = keep.tile([P, 1], F32)
+        nc.vector.tensor_scalar(
+            out=eps[:], in0=table_in[:], scalar1=0.0, scalar2=BN_EPS, op0=ALU.mult, op1=ALU.add
+        )
 
         cl_sb = keep.tile([P, PACK, K], BF16)
         for u in range(2):
@@ -61,23 +68,28 @@ def tile_modelnew_kernel(tc, x, clusters, clusters2, bn_gamma, bn_beta, out):
                 out=cl_sb[:, 2 * u : 2 * u + 2, :],
                 in_=clusters[256 * u : 256 * u + 256, :].rearrange("(q e) k -> q e k", e=2),
             )
+        nc.scalar.sqrt(table_out[:], table_in[:])
+
         c2_sb = keep.tile([P, D_BLOCKS, K], BF16)
-        nc.scalar.dma_start(out=c2_sb[:], in_=clusters2[0].rearrange("(t p) k -> p t k", p=P))
         gb_rows = keep.tile([P, P], BF16)
         nc.vector.memset(gb_rows[:], 0.0)
-        nc.scalar.dma_start(out=gb_rows[0:1, :], in_=bn_gamma.rearrange("(o k) -> o k", o=1))
-        nc.scalar.dma_start(out=gb_rows[1:2, :], in_=bn_beta.rearrange("(o k) -> o k", o=1))
-        nc.scalar.activation(out=table_out[:, 0:1], in_=table_in[:], func=ACT.Exp)
+
+        def load_small_inputs():
+            nc.sync.dma_start(out=c2_sb[:], in_=clusters2[0].rearrange("(t p) k -> p t k", p=P))
+            nc.sync.dma_start(out=gb_rows[0:1, :], in_=bn_gamma.rearrange("(o k) -> o k", o=1))
+            nc.sync.dma_start(out=gb_rows[1:2, :], in_=bn_beta.rearrange("(o k) -> o k", o=1))
 
         cl_grouped = keep.tile([P, K, PACK], BF16, align_bytes=64)
-        nc.vector.tensor_copy(out=cl_grouped[:], in_=cl_sb[:].rearrange("q t k -> q k t"))
         cl_codes = keep.tile([P, K], U32, align_bytes=64)
         cl_scales = keep.tile([P, K], U8, align_bytes=64)
-        nc.vector.quantize_mx(
-            out=cl_codes[:].bitcast(FP8X4),
-            scales=cl_scales[:],
-            in_=cl_grouped[:].rearrange("q k t -> q (k t)"),
-        )
+
+        def quantise_clusters():
+            nc.vector.tensor_copy(out=cl_grouped[:], in_=cl_sb[:].rearrange("q t k -> q k t"))
+            nc.vector.quantize_mx(
+                out=cl_codes[:].bitcast(FP8X4),
+                scales=cl_scales[:],
+                in_=cl_grouped[:].rearrange("q k t -> q (k t)"),
+            )
 
         c2T = keep.tile([P, D], F32)
         gb = keep.tile([P, 2], F32)
@@ -88,6 +100,7 @@ def tile_modelnew_kernel(tc, x, clusters, clusters2, bn_gamma, bn_beta, out):
         xn_scales = keep.tile([P, CHUNKS, D], U8, align_bytes=64)
         stats = keep.tile([P, CHUNKS, 6], F32)
         aT = {}
+        x_late, g_late = {}, {}
 
         def project(psum, c):
             aT[c] = psum.tile([P, K_PASS], F32, name="aT")
@@ -99,6 +112,47 @@ def tile_modelnew_kernel(tc, x, clusters, clusters2, bn_gamma, bn_beta, out):
                 rhs_scale=xd_scales[:, c, :],
                 start=True,
                 stop=True,
+            )
+
+        def load_late(c):
+            x_late[c] = late.tile([P, PACK, D_LATE], BF16, name="x_late")
+            nc.sync.dma_start(
+                out=x_late[c][:],
+                in_=x_rows[c * K_PASS : (c + 1) * K_PASS, D_EARLY:D].rearrange("(p j) d -> p j d", j=PACK),
+            )
+
+        def regroup_late(c, scalar_columns):
+            g_late[c] = late.tile([P, D_LATE, PACK], BF16, align_bytes=64, name="g_late")
+            dst = g_late[c][:].rearrange("p (c i) j -> p c j i", i=4)
+            src = x_late[c][:].rearrange("p j (c i) -> p c j i", i=4)
+            cut = scalar_columns // 4
+            if cut > 0:
+                nc.scalar.copy(out=dst[:, 0:cut], in_=src[:, 0:cut])
+            if cut < D_LATE // 4:
+                nc.vector.tensor_copy(out=dst[:, cut:], in_=src[:, cut:])
+
+        def quantise_late(c):
+            nc.vector.quantize_mx(
+                out=xn_codes[:, c, D_EARLY:D].bitcast(FP8X4),
+                scales=xn_scales[:, c, D_EARLY:D],
+                in_=g_late[c][:].rearrange("p d j -> p (d j)"),
+            )
+
+        mean_var = keep.tile([P, 2], F32)
+        std = keep.tile([P, 1], F32)
+        neg_mean = keep.tile([P, 1], F32)
+        rstd = keep.tile([P, 1], F32)
+        bn_scale = keep.tile([P, 1], F32)
+        bn_shift = keep.tile([P, 1], F32)
+
+        def batch_norm_vectors():
+            nc.vector.bn_aggr(out=mean_var[:], in_=stats[:].rearrange("p c s -> p (c s)"))
+            nc.scalar.activation(out=std[:], in_=mean_var[:, 1:2], func=ACT.Sqrt, bias=eps[:, 0:1], scale=1.0)
+            nc.vector.tensor_scalar_mul(out=neg_mean[:], in0=mean_var[:, 0:1], scalar1=-1.0)
+            nc.vector.reciprocal(rstd[:], std[:])
+            nc.vector.tensor_mul(out=bn_scale[:], in0=gb[:, 0:1], in1=rstd[:])
+            nc.vector.scalar_tensor_tensor(
+                out=bn_shift[:], in0=neg_mean[:], scalar=bn_scale[:, 0:1], in1=gb[:, 1:2], op0=ALU.mult, op1=ALU.add
             )
 
         with ExitStack() as ph1:
@@ -120,10 +174,13 @@ def tile_modelnew_kernel(tc, x, clusters, clusters2, bn_gamma, bn_beta, out):
 
             def load(c):
                 x_sb[c] = xin.tile([P, PACK, D], BF16, name="x_sb")
-                nc.sync.dma_start(
-                    out=x_sb[c][:],
-                    in_=x_rows[c * K_PASS : (c + 1) * K_PASS, :].rearrange("(p j) d -> p j d", j=PACK),
-                )
+                src = x_rows[c * K_PASS : (c + 1) * K_PASS, :].rearrange("(p j) d -> p j d", j=PACK)
+                pieces = 2 if c == 0 else 1
+                rows = PACK // pieces
+                for i in range(pieces):
+                    nc.sync.dma_start(
+                        out=x_sb[c][:, i * rows : (i + 1) * rows, :], in_=src[:, i * rows : (i + 1) * rows, :]
+                    )
 
             def transpose_words(c):
                 x_words = x_sb[c][:].bitcast(F32)
@@ -171,79 +228,52 @@ def tile_modelnew_kernel(tc, x, clusters, clusters2, bn_gamma, bn_beta, out):
                         in_=gn[c][:, cols, :].rearrange("p d j -> p (d j)"),
                     )
 
+            def statistics(c):
+                nc.vector.bn_stats(out=stats[:, c, :], in_=aT[c][:])
+
             for s in range(-LOAD_AHEAD, CHUNKS + 2):
                 if live(s + LOAD_AHEAD):
                     load(s + LOAD_AHEAD)
+                if s == -1:
+                    load_small_inputs()
+                if CHUNKS <= s + LOAD_AHEAD < CHUNKS + LATE_FILL // 2:
+                    load_late(2 * (s + LOAD_AHEAD - CHUNKS))
+                    load_late(2 * (s + LOAD_AHEAD - CHUNKS) + 1)
                 if live(s + 1):
                     transpose_words(s + 1)
                 if s == SETUP_STEP:
                     transpose_small_inputs()
+                if s == 0:
+                    quantise_clusters()
                 if live(s - 1):
                     quantise_along_d(s - 1)
                     project(ps_a1, s - 1)
                 if live(s):
                     copy_words(s)
                     regroup(s)
-                if live(s - 1):
+                if live(s - 1) and s - 1 < CHUNKS - 2:
                     quantise_along_n(s - 1)
                 if live(s - 2):
-                    nc.vector.bn_stats(out=stats[:, s - 2, :], in_=aT[s - 2][:])
-
-        mean_var = keep.tile([P, 2], F32)
-        nc.vector.bn_aggr(out=mean_var[:], in_=stats[:].rearrange("p c s -> p (c s)"))
-        neg_half = keep.tile([P, 1], F32)
-        nc.gpsimd.memset(neg_half[:], -0.5)
-        var_eps = keep.tile([P, 1], F32)
-        nc.vector.tensor_scalar_add(out=var_eps[:], in0=mean_var[:, 1:2], scalar1=BN_EPS)
-        neg_mean = keep.tile([P, 1], F32)
-        nc.vector.tensor_scalar_mul(out=neg_mean[:], in0=mean_var[:, 0:1], scalar1=-1.0)
-        rstd = keep.tile([P, 1], F32)
-        nc.gpsimd.tensor_tensor(out=rstd[:], in0=var_eps[:], in1=neg_half[:], op=ALU.pow)
-        bn_scale = keep.tile([P, 1], F32)
-        nc.vector.tensor_mul(out=bn_scale[:], in0=gb[:, 0:1], in1=rstd[:])
-        bn_shift = keep.tile([P, 1], F32)
-        nc.vector.scalar_tensor_tensor(
-            out=bn_shift[:], in0=neg_mean[:], scalar=bn_scale[:, 0:1], in1=gb[:, 1:2], op0=ALU.mult, op1=ALU.add
-        )
+                    statistics(s - 2)
+            for c in range(LATE_FILL):
+                regroup_late(c, D_LATE)
+            batch_norm_vectors()
+            for c in (CHUNKS - 2, CHUNKS - 1):
+                quantise_along_n(c)
+            for c in range(LATE_FILL):
+                quantise_late(c)
 
         with ExitStack() as ph2:
             work = ph2.enter_context(tc.tile_pool(name="work", bufs=3))
-            rows = ph2.enter_context(tc.tile_pool(name="rows", bufs=4))
-            late = ph2.enter_context(tc.tile_pool(name="late", bufs=LOAD_AHEAD + 2))
-            outs = ph2.enter_context(tc.tile_pool(name="outs", bufs=3))
+            outs = ph2.enter_context(tc.tile_pool(name="outs", bufs=2))
             norms = ph2.enter_context(tc.tile_pool(name="norms", bufs=3))
-            x_late, g_late = {}, {}
             ps_a2 = ph2.enter_context(tc.psum_pool(name="ps_a2", bufs=2))
             ps_z = ph2.enter_context(tc.psum_pool(name="ps_z", bufs=3))
             ps_v = ph2.enter_context(tc.psum_pool(name="ps_v", bufs=2))
             ps_s = ph2.enter_context(tc.psum_pool(name="ps_s", bufs=1))
-            v, sumsq, inv1, total_sb, factor, scaled, oT = {}, {}, {}, {}, {}, {}, {}
             zT, z, neg_max, e, row_sum, inv_sum, pf, pg, p_codes, p_scales, vT = {}, {}, {}, {}, {}, {}, {}, {}, {}, {}, {}
+            v, sumsq, norm_sq, inv1_sq, inv_norm, scaled, oT = {}, {}, {}, {}, {}, {}, {}
             p_sums = ps_s.tile([P, 4, P], F32)
-
-            def load_late(c):
-                x_late[c] = late.tile([P, PACK, D_LATE], BF16, name="x_late")
-                nc.sync.dma_start(
-                    out=x_late[c][:],
-                    in_=x_rows[c * K_PASS : (c + 1) * K_PASS, D_EARLY:D].rearrange("(p j) d -> p j d", j=PACK),
-                )
-
-            def regroup_late(c):
-                g_late[c] = late.tile([P, D_LATE, PACK], BF16, align_bytes=64, name="g_late")
-                dst = g_late[c][:].rearrange("p (c i) j -> p c j i", i=4)
-                late_src = x_late[c][:].rearrange("p j (c i) -> p c j i", i=4)
-                cut = SCALAR_LATE // 4
-                if cut > 0:
-                    nc.scalar.copy(out=dst[:, 0:cut], in_=late_src[:, 0:cut])
-                if cut < D_LATE // 4:
-                    nc.vector.tensor_copy(out=dst[:, cut:], in_=late_src[:, cut:])
-
-            def quantise_late(c):
-                nc.vector.quantize_mx(
-                    out=xn_codes[:, c, D_EARLY:D].bitcast(FP8X4),
-                    scales=xn_scales[:, c, D_EARLY:D],
-                    in_=g_late[c][:].rearrange("p d j -> p (d j)"),
-                )
 
             def normalise(c):
                 zT[c] = work.tile([P, K_PASS], F32, name="zT")
@@ -261,8 +291,8 @@ def tile_modelnew_kernel(tc, x, clusters, clusters2, bn_gamma, bn_beta, out):
                 nc.vector.tensor_reduce(out=neg_max[c][:], in_=z[c][:], axis=AX.X, op=ALU.max, negate=True)
 
             def exponentials(c):
-                e[c] = rows.tile([P, PACK, K], F32, name="e")
-                row_sum[c] = rows.tile([P, PACK], F32, name="row_sum")
+                e[c] = work.tile([P, PACK, K], F32, name="e")
+                row_sum[c] = work.tile([P, PACK], F32, name="row_sum")
                 for j in range(PACK):
                     nc.scalar.activation(
                         out=e[c][:, j, :],
@@ -274,7 +304,7 @@ def tile_modelnew_kernel(tc, x, clusters, clusters2, bn_gamma, bn_beta, out):
                     )
 
             def invert_sums(c):
-                inv_sum[c] = rows.tile([P, PACK], F32, name="inv_sum")
+                inv_sum[c] = work.tile([P, PACK], F32, name="inv_sum")
                 nc.vector.reciprocal(inv_sum[c][:], row_sum[c][:])
 
             def probabilities(c):
@@ -336,38 +366,40 @@ def tile_modelnew_kernel(tc, x, clusters, clusters2, bn_gamma, bn_beta, out):
             def sum_of_squares(b):
                 squares = outs.tile([P, D], F32, name="squares")
                 sumsq[b] = norms.tile([P, 1], F32, name="sumsq")
-                nc.scalar.activation(out=squares[:], in_=v[b][:], func=ACT.Square, accum_out=sumsq[b][:, 0:1])
+                nc.scalar.activation(out=squares[:], in_=v[b][:], func=ACT.Square, accum_out=sumsq[b][:])
 
-            def rsqrt_floored(out_tile, x):
-                nc.gpsimd.tensor_tensor(out=out_tile[:], in0=x[:], in1=neg_half[:], op=ALU.pow)
+            def floor_columns(b):
+                norm_sq[b] = norms.tile([P, 2], F32, name="norm_sq")
+                nc.vector.tensor_scalar_max(out=norm_sq[b][:, 0:1], in0=sumsq[b][:], scalar1=NORM_EPS * NORM_EPS)
 
-            def column_norms(b):
-                floored = norms.tile([P, 1], F32, name="floored")
-                nc.gpsimd.tensor_scalar(
-                    out=floored[:], in0=sumsq[b][:], scalar1=NORM_EPS * NORM_EPS, scalar2=None, op0=ALU.max
-                )
-                inv1[b] = norms.tile([P, 1], F32, name="inv1")
-                rsqrt_floored(inv1[b], floored)
-                part = norms.tile([P, 1], F32, name="part")
-                nc.gpsimd.tensor_tensor(out=part[:], in0=sumsq[b][:], in1=inv1[b][:], op=ALU.mult)
-                part2 = norms.tile([P, 1], F32, name="part2")
-                nc.gpsimd.tensor_tensor(out=part2[:], in0=part[:], in1=inv1[b][:], op=ALU.mult)
-                total_sb[b] = part2
+            def invert_columns(b):
+                inv1_sq[b] = norms.tile([P, 1], F32, name="inv1_sq")
+                nc.vector.reciprocal(inv1_sq[b][:], norm_sq[b][:, 0:1])
 
             def row_total(b):
-                nc.tensor.matmul(out=vT[b][:, 0:1], lhsT=ones_f32[:], rhs=total_sb[b][:], start=True, stop=True)
+                nc.tensor.matmul(
+                    out=vT[b][:, 0:1],
+                    lhsT=sumsq[b][:, 0:1].to_broadcast([P, P]),
+                    rhs=inv1_sq[b][:],
+                    start=True,
+                    stop=True,
+                )
 
-            def row_norm(b):
-                total = norms.tile([P, 1], F32, name="total")
-                nc.vector.tensor_scalar_max(out=total[:], in0=vT[b][:, 0:1], scalar1=NORM_EPS * NORM_EPS)
-                inv2 = norms.tile([P, 1], F32, name="inv2")
-                rsqrt_floored(inv2, total)
-                factor[b] = norms.tile([P, 1], F32, name="factor")
-                nc.gpsimd.tensor_tensor(out=factor[b][:], in0=inv2[:], in1=inv1[b][:], op=ALU.mult)
+            def invert_norms(b):
+                nc.vector.tensor_scalar_max(out=norm_sq[b][:, 1:2], in0=vT[b][:, 0:1], scalar1=NORM_EPS * NORM_EPS)
+                inv_norm[b] = norms.tile([P, 2], F32, name="inv_norm")
+                nc.gpsimd.tensor_tensor(out=inv_norm[b][:], in0=norm_sq[b][:], in1=neg_half[:], op=ALU.pow)
 
             def scale_rows(b):
                 scaled[b] = outs.tile([P, D], F32, name="scaled")
-                nc.vector.tensor_scalar_mul(out=scaled[b][:], in0=v[b][:], scalar1=factor[b][:, 0:1])
+                nc.vector.tensor_scalar(
+                    out=scaled[b][:],
+                    in0=v[b][:],
+                    scalar1=inv_norm[b][:, 0:1],
+                    scalar2=inv_norm[b][:, 1:2],
+                    op0=ALU.mult,
+                    op1=ALU.mult,
+                )
 
             def to_out(b):
                 oT[b] = ps_z.tile([P, D_BLOCKS, K], F32, name="z")
@@ -380,49 +412,61 @@ def tile_modelnew_kernel(tc, x, clusters, clusters2, bn_gamma, bn_beta, out):
                 nc.sync.dma_start(out=out[b].rearrange("(t p k) -> p t k", t=D_BLOCKS, p=P), in_=o_sb[:])
 
             def batch_at(s, lag):
-                c = s - 3 - lag
-                return c // CHUNKS_PER_BATCH if live(c) and c % CHUNKS_PER_BATCH == CHUNKS_PER_BATCH - 1 else None
+                b, cc = divmod(s - 3 - lag, CHUNKS_PER_BATCH)
+                return b if live(s - 3 - lag) and cc == CHUNKS_PER_BATCH - 1 else None
 
-            for s in range(-LOAD_AHEAD, CHUNKS + 3 + 7):
-                if live(s + LOAD_AHEAD):
-                    load_late(s + LOAD_AHEAD)
-                done = [batch_at(s, lag) for lag in range(7)]
+            late_chunk = LATE_FILL
+            waiting = []
+            for c in range(LATE_FILL, LATE_FILL + 2):
+                load_late(c)
+            for s in range(-LOAD_AHEAD, CHUNKS + 3 + TAIL):
+                done = [batch_at(s, lag) for lag in range(TAIL)]
+                if live(s + 2):
+                    to_rows(s + 2)
+                if done[6] is not None:
+                    to_out(done[6])
+                if done[3] is not None:
+                    row_total(done[3])
+                if live(s - 2):
+                    sum_of_p(s - 2)
                 if live(s - 3):
                     pool_chunk(s - 3)
                 if live(s + 4):
                     project(ps_a2, s + 4)
-                if done[2] is not None:
-                    row_total(done[2])
-                if live(s + 2):
-                    to_rows(s + 2)
-                if done[5] is not None:
-                    to_out(done[5])
                 if live(s + 3):
                     normalise(s + 3)
-                if live(s - 2):
-                    sum_of_p(s - 2)
+                if done[2] is not None:
+                    floor_columns(done[2])
                 if live(s - 1):
                     invert_sums(s - 1)
                 if live(s + 1):
                     row_max(s + 1)
+                if done[2] is not None:
+                    invert_columns(done[2])
                 if live(s - 1):
                     probabilities(s - 1)
                 if done[0] is not None:
                     subtract_centres(done[0])
                 if done[3] is not None:
-                    row_norm(done[3])
-                if done[4] is not None:
-                    scale_rows(done[4])
+                    invert_norms(done[3])
+                if done[5] is not None:
+                    scale_rows(done[5])
                 if live(s - 2):
                     quantise_p(s - 2)
                 if live(s - 1):
                     round_p(s - 1)
-                    quantise_late(s - 1)
-                if done[1] is not None:
-                    sum_of_squares(done[1])
-                    column_norms(done[1])
+                for c in waiting:
+                    quantise_late(c)
+                waiting = []
                 if live(s):
                     exponentials(s)
-                    regroup_late(s)
-                if done[6] is not None:
-                    store(done[6])
+                if done[1] is not None:
+                    sum_of_squares(done[1])
+                if s >= 0 and done[0] is None and live(late_chunk):
+                    if live(late_chunk + 2):
+                        load_late(late_chunk + 2)
+                    regroup_late(late_chunk, SCALAR_LATE)
+                    waiting.append(late_chunk)
+                    late_chunk += 1
+                if done[7] is not None:
+                    store(done[7])

@@ -28,9 +28,10 @@ D_CALL = 256
 SCALAR_D = 208
 SCALAR_LATE = 96
 LOAD_AHEAD = 4
+LATE_AHEAD = 5
 LATE_FILL = 6
 SETUP_STEP = 2
-TAIL = 8
+TAIL = 9
 
 FLOPS = 2 * 2 * ROWS * D * K
 
@@ -272,7 +273,7 @@ def tile_modelnew_kernel(tc, x, clusters, clusters2, bn_gamma, bn_beta, out):
             ps_v = ph2.enter_context(tc.psum_pool(name="ps_v", bufs=2))
             ps_s = ph2.enter_context(tc.psum_pool(name="ps_s", bufs=1))
             zT, z, neg_max, e, row_sum, inv_sum, pf, pg, p_codes, p_scales, vT = {}, {}, {}, {}, {}, {}, {}, {}, {}, {}, {}
-            v, sumsq, norm_sq, inv1_sq, inv_norm, scaled, oT = {}, {}, {}, {}, {}, {}, {}
+            v, sumsq, norm_sq, inv1_sq, inv_norm, scaled, oT, o_sb = {}, {}, {}, {}, {}, {}, {}, {}
             p_sums = ps_s.tile([P, 4, P], F32)
 
             def normalise(c):
@@ -406,10 +407,12 @@ def tile_modelnew_kernel(tc, x, clusters, clusters2, bn_gamma, bn_beta, out):
                 for t in range(D_BLOCKS):
                     nc.tensor.transpose(oT[b][:, t, :], scaled[b][:, t * P : (t + 1) * P], ident_f32[:])
 
+            def copy_out(b):
+                o_sb[b] = outs.tile([P, D_BLOCKS, K], F32, name="o_sb")
+                nc.scalar.copy(out=o_sb[b][:], in_=oT[b][:])
+
             def store(b):
-                o_sb = outs.tile([P, D_BLOCKS, K], F32, name="o_sb")
-                nc.scalar.copy(out=o_sb[:], in_=oT[b][:])
-                nc.sync.dma_start(out=out[b].rearrange("(t p k) -> p t k", t=D_BLOCKS, p=P), in_=o_sb[:])
+                nc.scalar.dma_start(out=out[b].rearrange("(t p k) -> p t k", t=D_BLOCKS, p=P), in_=o_sb[b][:])
 
             def batch_at(s, lag):
                 b, cc = divmod(s - 3 - lag, CHUNKS_PER_BATCH)
@@ -417,22 +420,22 @@ def tile_modelnew_kernel(tc, x, clusters, clusters2, bn_gamma, bn_beta, out):
 
             late_chunk = LATE_FILL
             waiting = []
-            for c in range(LATE_FILL, LATE_FILL + 2):
+            for c in range(LATE_FILL, LATE_FILL + LATE_AHEAD):
                 load_late(c)
             for s in range(-LOAD_AHEAD, CHUNKS + 3 + TAIL):
                 done = [batch_at(s, lag) for lag in range(TAIL)]
-                if live(s + 2):
-                    to_rows(s + 2)
-                if done[6] is not None:
-                    to_out(done[6])
-                if done[3] is not None:
-                    row_total(done[3])
-                if live(s - 2):
-                    sum_of_p(s - 2)
                 if live(s - 3):
                     pool_chunk(s - 3)
                 if live(s + 4):
                     project(ps_a2, s + 4)
+                if done[3] is not None:
+                    row_total(done[3])
+                if live(s + 2):
+                    to_rows(s + 2)
+                if done[6] is not None:
+                    to_out(done[6])
+                if live(s - 2):
+                    sum_of_p(s - 2)
                 if live(s + 3):
                     normalise(s + 3)
                 if done[2] is not None:
@@ -463,10 +466,12 @@ def tile_modelnew_kernel(tc, x, clusters, clusters2, bn_gamma, bn_beta, out):
                 if done[1] is not None:
                     sum_of_squares(done[1])
                 if s >= 0 and done[0] is None and live(late_chunk):
-                    if live(late_chunk + 2):
-                        load_late(late_chunk + 2)
+                    if live(late_chunk + LATE_AHEAD):
+                        load_late(late_chunk + LATE_AHEAD)
                     regroup_late(late_chunk, SCALAR_LATE)
                     waiting.append(late_chunk)
                     late_chunk += 1
+                if done[8] is not None:
+                    store(done[8])
                 if done[7] is not None:
-                    store(done[7])
+                    copy_out(done[7])

@@ -29,9 +29,9 @@ SCALAR_D = 208
 SCALAR_LATE = 96
 LOAD_AHEAD = 4
 LATE_AHEAD = 5
+LATE_VECTOR = 2
 LATE_FILL = 6
 SETUP_STEP = 2
-TAIL = 9
 
 FLOPS = 2 * 2 * ROWS * D * K
 
@@ -47,17 +47,17 @@ def tile_modelnew_kernel(tc, x, clusters, clusters2, bn_gamma, bn_beta, out):
     with ExitStack() as ctx:
         ctx.enter_context(tc.manual_schedule())
         keep = ctx.enter_context(tc.tile_pool(name="keep", bufs=1))
-        late = ctx.enter_context(tc.tile_pool(name="late", bufs=LATE_FILL + 4))
+        late = ctx.enter_context(tc.tile_pool(name="late", bufs=LATE_FILL + LATE_VECTOR + 1))
 
         ident_f32 = keep.tile([P, P], F32)
         make_identity(nc, ident_f32[:])
         ident_bf16 = keep.tile([P, P], BF16)
         make_identity(nc, ident_bf16[:])
+        ones_f32 = keep.tile([P, P], F32)
+        nc.vector.memset(ones_f32[:], 1.0)
         table_in = keep.tile([P, 1], F32)
         nc.vector.memset(table_in[:], 1.0)
         table_out = keep.tile([P, 1], F32)
-        neg_half = keep.tile([P, 2], F32)
-        nc.vector.memset(neg_half[:], -0.5)
         eps = keep.tile([P, 1], F32)
         nc.vector.tensor_scalar(
             out=eps[:], in0=table_in[:], scalar1=0.0, scalar2=BN_EPS, op0=ALU.mult, op1=ALU.add
@@ -116,7 +116,7 @@ def tile_modelnew_kernel(tc, x, clusters, clusters2, bn_gamma, bn_beta, out):
             )
 
         def load_late(c):
-            x_late[c] = late.tile([P, PACK, D_LATE], BF16, name="x_late")
+            x_late[c] = late.tile([P, PACK, D_LATE], BF16, name="x_late", bufs=6)
             nc.sync.dma_start(
                 out=x_late[c][:],
                 in_=x_rows[c * K_PASS : (c + 1) * K_PASS, D_EARLY:D].rearrange("(p j) d -> p j d", j=PACK),
@@ -159,6 +159,7 @@ def tile_modelnew_kernel(tc, x, clusters, clusters2, bn_gamma, bn_beta, out):
         with ExitStack() as ph1:
             xin = ph1.enter_context(tc.tile_pool(name="xin", bufs=LOAD_AHEAD + 2))
             grp = ph1.enter_context(tc.tile_pool(name="grp", bufs=3))
+            grn = ph1.enter_context(tc.tile_pool(name="grn", bufs=4))
             ps_set = ph1.enter_context(tc.psum_pool(name="ps_set", bufs=1))
             ps_xt = ph1.enter_context(tc.psum_pool(name="ps_xt", bufs=4))
             ps_a1 = ph1.enter_context(tc.psum_pool(name="ps_a1", bufs=2))
@@ -214,12 +215,24 @@ def tile_modelnew_kernel(tc, x, clusters, clusters2, bn_gamma, bn_beta, out):
                 )
 
             def regroup(c):
-                gn[c] = grp.tile([P, D_EARLY, PACK], BF16, align_bytes=64, name="gn")
+                scalar_part(c)
+                vector_part(c)
+
+            def scalar_part(c):
+                gn[c] = grn.tile([P, D_EARLY, PACK], BF16, align_bytes=64, name="gn")
+                regroup_part(c, nc.scalar)
+
+            def vector_part(c):
+                regroup_part(c, nc.vector)
+
+            def regroup_part(c, engine):
                 dst = gn[c][:].rearrange("p (c i) j -> p c j i", i=4)
                 src = x_sb[c][:, :, 0:D_EARLY].rearrange("p j (c i) -> p c j i", i=4)
                 cut = SCALAR_D // 4
-                nc.scalar.copy(out=dst[:, 0:cut], in_=src[:, 0:cut])
-                nc.vector.tensor_copy(out=dst[:, cut:], in_=src[:, cut:])
+                if engine is nc.scalar:
+                    nc.scalar.copy(out=dst[:, 0:cut], in_=src[:, 0:cut])
+                else:
+                    nc.vector.tensor_copy(out=dst[:, cut:], in_=src[:, cut:])
 
             def quantise_along_n(c):
                 for cols in (slice(0, D_CALL), slice(D_CALL, D_EARLY)):
@@ -237,7 +250,7 @@ def tile_modelnew_kernel(tc, x, clusters, clusters2, bn_gamma, bn_beta, out):
                     load(s + LOAD_AHEAD)
                 if s == -1:
                     load_small_inputs()
-                if CHUNKS <= s + LOAD_AHEAD < CHUNKS + LATE_FILL // 2:
+                if CHUNKS <= s + LOAD_AHEAD < CHUNKS + (LATE_FILL + LATE_VECTOR) // 2:
                     load_late(2 * (s + LOAD_AHEAD - CHUNKS))
                     load_late(2 * (s + LOAD_AHEAD - CHUNKS) + 1)
                 if live(s + 1):
@@ -251,30 +264,35 @@ def tile_modelnew_kernel(tc, x, clusters, clusters2, bn_gamma, bn_beta, out):
                     project(ps_a1, s - 1)
                 if live(s):
                     copy_words(s)
-                    regroup(s)
-                if live(s - 1) and s - 1 < CHUNKS - 2:
+                    if s < CHUNKS - 1:
+                        regroup(s)
+                if live(s - 1) and s - 1 < CHUNKS - 3:
                     quantise_along_n(s - 1)
                 if live(s - 2):
                     statistics(s - 2)
+            scalar_part(CHUNKS - 1)
             for c in range(LATE_FILL):
                 regroup_late(c, D_LATE)
             batch_norm_vectors()
-            for c in (CHUNKS - 2, CHUNKS - 1):
+            vector_part(CHUNKS - 1)
+            for c in range(CHUNKS - 3, CHUNKS):
                 quantise_along_n(c)
-            for c in range(LATE_FILL):
-                quantise_late(c)
 
         with ExitStack() as ph2:
             work = ph2.enter_context(tc.tile_pool(name="work", bufs=3))
-            outs = ph2.enter_context(tc.tile_pool(name="outs", bufs=2))
-            norms = ph2.enter_context(tc.tile_pool(name="norms", bufs=3))
+            outs = ph2.enter_context(tc.tile_pool(name="outs", bufs=3))
+            norms = ph2.enter_context(tc.tile_pool(name="norms", bufs=2))
             ps_a2 = ph2.enter_context(tc.psum_pool(name="ps_a2", bufs=2))
             ps_z = ph2.enter_context(tc.psum_pool(name="ps_z", bufs=3))
-            ps_v = ph2.enter_context(tc.psum_pool(name="ps_v", bufs=2))
+            ps_v = ph2.enter_context(tc.psum_pool(name="ps_v", bufs=1))
             ps_s = ph2.enter_context(tc.psum_pool(name="ps_s", bufs=1))
             zT, z, neg_max, e, row_sum, inv_sum, pf, pg, p_codes, p_scales, vT = {}, {}, {}, {}, {}, {}, {}, {}, {}, {}, {}
-            v, sumsq, norm_sq, inv1_sq, inv_norm, scaled, oT, o_sb = {}, {}, {}, {}, {}, {}, {}, {}
-            p_sums = ps_s.tile([P, 4, P], F32)
+            scaled, oT, neg_asum = {}, {}, {}
+            v = outs.tile([P, B, D], F32, bufs=1)
+            sumsq = norms.tile([P, B], F32, bufs=1)
+            s_even = ps_s.tile([P, 4, P], F32, name="s_even")
+            s_odd = ps_s.tile([P, 4, P], F32, name="s_odd")
+            s_bank = [s_even, s_odd]
 
             def normalise(c):
                 zT[c] = work.tile([P, K_PASS], F32, name="zT")
@@ -323,7 +341,7 @@ def tile_modelnew_kernel(tc, x, clusters, clusters2, bn_gamma, bn_beta, out):
                 b, cc = divmod(c, CHUNKS_PER_BATCH)
                 for j in range(PACK):
                     nc.tensor.matmul(
-                        out=p_sums[:, b % 4, :],
+                        out=s_bank[b % 2][:, 0, :],
                         lhsT=pf[c][:, j, :],
                         rhs=ident_f32[:],
                         is_transpose=True,
@@ -354,48 +372,62 @@ def tile_modelnew_kernel(tc, x, clusters, clusters2, bn_gamma, bn_beta, out):
                     stop=(cc == CHUNKS_PER_BATCH - 1),
                 )
 
-            def subtract_centres(b):
-                neg_asum = norms.tile([P, 1], F32, name="neg_asum")
+            def total_of_p(b):
+                neg_asum[b] = norms.tile([P, 1], F32, name="neg_asum")
                 nc.vector.tensor_reduce(
-                    out=neg_asum[:], in_=p_sums[:, b % 4, :], axis=AX.X, op=ALU.add, negate=True
+                    out=neg_asum[b][:], in_=s_bank[b % 2][:, 0, :], axis=AX.X, op=ALU.add, negate=True
                 )
-                v[b] = outs.tile([P, D], F32, name="v")
+
+            def pooled_minus_centres(b):
                 nc.vector.scalar_tensor_tensor(
-                    out=v[b][:], in0=c2T[:], scalar=neg_asum[:, 0:1], in1=vT[b][:], op0=ALU.mult, op1=ALU.add
+                    out=v[:, b, :], in0=c2T[:], scalar=neg_asum[b][:, 0:1], in1=vT[b][:], op0=ALU.mult, op1=ALU.add
                 )
 
             def sum_of_squares(b):
-                squares = outs.tile([P, D], F32, name="squares")
-                sumsq[b] = norms.tile([P, 1], F32, name="sumsq")
-                nc.scalar.activation(out=squares[:], in_=v[b][:], func=ACT.Square, accum_out=sumsq[b][:])
+                squares = outs.tile([P, D], F32, name="scaled")
+                nc.scalar.activation(out=squares[:], in_=v[:, b, :], func=ACT.Square, accum_out=sumsq[:, b : b + 1])
 
-            def floor_columns(b):
-                norm_sq[b] = norms.tile([P, 2], F32, name="norm_sq")
-                nc.vector.tensor_scalar_max(out=norm_sq[b][:, 0:1], in0=sumsq[b][:], scalar1=NORM_EPS * NORM_EPS)
+            norm_sq, col_inv, share, norm, inv_norm = {}, {}, {}, {}, {}
 
-            def invert_columns(b):
-                inv1_sq[b] = norms.tile([P, 1], F32, name="inv1_sq")
-                nc.vector.reciprocal(inv1_sq[b][:], norm_sq[b][:, 0:1])
-
-            def row_total(b):
-                nc.tensor.matmul(
-                    out=vT[b][:, 0:1],
-                    lhsT=sumsq[b][:, 0:1].to_broadcast([P, P]),
-                    rhs=inv1_sq[b][:],
-                    start=True,
-                    stop=True,
+            def floor_columns(lo, hi):
+                norm_sq[lo] = norms.tile([P, 2, hi - lo], F32, name="norm_sq%d" % lo)
+                nc.vector.tensor_scalar_max(
+                    out=norm_sq[lo][:, 0, :], in0=sumsq[:, lo:hi], scalar1=NORM_EPS * NORM_EPS
                 )
 
-            def invert_norms(b):
-                nc.vector.tensor_scalar_max(out=norm_sq[b][:, 1:2], in0=vT[b][:, 0:1], scalar1=NORM_EPS * NORM_EPS)
-                inv_norm[b] = norms.tile([P, 2], F32, name="inv_norm")
-                nc.gpsimd.tensor_tensor(out=inv_norm[b][:], in0=norm_sq[b][:], in1=neg_half[:], op=ALU.pow)
+            def invert_columns(lo, hi):
+                col_inv[lo] = norms.tile([P, hi - lo], F32, name="col_inv%d" % lo)
+                nc.vector.reciprocal(col_inv[lo][:], norm_sq[lo][:, 0, :])
+
+            def column_shares(lo, hi):
+                share[lo] = norms.tile([P, hi - lo], F32, name="share%d" % lo)
+                nc.vector.tensor_mul(out=share[lo][:], in0=sumsq[:, lo:hi], in1=col_inv[lo][:])
+
+            def row_totals(lo, hi):
+                nc.tensor.matmul(
+                    out=s_bank[0][:, 1, lo:hi], lhsT=ones_f32[:], rhs=share[lo][:], start=True, stop=True
+                )
+
+            def floor_rows(lo, hi):
+                nc.vector.tensor_scalar_max(
+                    out=norm_sq[lo][:, 1, :], in0=s_bank[0][:, 1, lo:hi], scalar1=NORM_EPS * NORM_EPS
+                )
+
+            def take_roots(lo, hi):
+                norm[lo] = norms.tile([P, 2, hi - lo], F32, name="norm%d" % lo)
+                nc.scalar.sqrt(norm[lo][:], norm_sq[lo][:])
+
+            def invert_norms(lo, hi):
+                inv = norms.tile([P, 2, hi - lo], F32, name="inv_norm%d" % lo)
+                nc.vector.reciprocal(inv[:], norm[lo][:])
+                for b in range(lo, hi):
+                    inv_norm[b] = inv[:, :, b - lo]
 
             def scale_rows(b):
                 scaled[b] = outs.tile([P, D], F32, name="scaled")
                 nc.vector.tensor_scalar(
                     out=scaled[b][:],
-                    in0=v[b][:],
+                    in0=v[:, b, :],
                     scalar1=inv_norm[b][:, 0:1],
                     scalar2=inv_norm[b][:, 1:2],
                     op0=ALU.mult,
@@ -407,71 +439,126 @@ def tile_modelnew_kernel(tc, x, clusters, clusters2, bn_gamma, bn_beta, out):
                 for t in range(D_BLOCKS):
                     nc.tensor.transpose(oT[b][:, t, :], scaled[b][:, t * P : (t + 1) * P], ident_f32[:])
 
-            def copy_out(b):
-                o_sb[b] = outs.tile([P, D_BLOCKS, K], F32, name="o_sb")
-                nc.scalar.copy(out=o_sb[b][:], in_=oT[b][:])
+            def o_sb(b):
+                return v[:, b, :].rearrange("p (t k) -> p t k", t=D_BLOCKS)
 
-            def store(b):
-                nc.scalar.dma_start(out=out[b].rearrange("(t p k) -> p t k", t=D_BLOCKS, p=P), in_=o_sb[b][:])
+            def copy_out(b, copy, blocks):
+                copy(out=o_sb(b)[:, blocks, :], in_=oT[b][:, blocks, :])
 
-            def batch_at(s, lag):
-                b, cc = divmod(s - 3 - lag, CHUNKS_PER_BATCH)
-                return b if live(s - 3 - lag) and cc == CHUNKS_PER_BATCH - 1 else None
+            def store(b, blocks):
+                nc.sync.dma_start(
+                    out=out[b].rearrange("(t p k) -> p t k", t=D_BLOCKS, p=P)[:, blocks, :], in_=o_sb(b)[:, blocks, :]
+                )
 
-            late_chunk = LATE_FILL
+            late_chunk = LATE_FILL + LATE_VECTOR
             waiting = []
-            for c in range(LATE_FILL, LATE_FILL + LATE_AHEAD):
+            for c in range(LATE_FILL + LATE_VECTOR, LATE_FILL + LATE_VECTOR + LATE_AHEAD):
                 load_late(c)
-            for s in range(-LOAD_AHEAD, CHUNKS + 3 + TAIL):
-                done = [batch_at(s, lag) for lag in range(TAIL)]
+            for s in range(-LOAD_AHEAD, CHUNKS + 2):
+                b, cc = divmod(s - 3, CHUNKS_PER_BATCH)
+                batch_done = live(s - 3) and cc == CHUNKS_PER_BATCH - 1
+                if s < 3 and live(s + 2):
+                    to_rows(s + 2)
                 if live(s - 3):
                     pool_chunk(s - 3)
                 if live(s + 4):
                     project(ps_a2, s + 4)
-                if done[3] is not None:
-                    row_total(done[3])
-                if live(s + 2):
+                if s == CHUNKS + 1:
+                    row_totals(0, B - 1)
+                if s >= 3 and live(s + 2):
                     to_rows(s + 2)
-                if done[6] is not None:
-                    to_out(done[6])
                 if live(s - 2):
                     sum_of_p(s - 2)
-                if live(s + 3):
-                    normalise(s + 3)
-                if done[2] is not None:
-                    floor_columns(done[2])
                 if live(s - 1):
                     invert_sums(s - 1)
                 if live(s + 1):
                     row_max(s + 1)
-                if done[2] is not None:
-                    invert_columns(done[2])
+                if s == -1:
+                    for c in range(LATE_FILL, LATE_FILL + LATE_VECTOR):
+                        regroup_late(c, 0)
+                if s == 0:
+                    for c in range(LATE_FILL + LATE_VECTOR):
+                        quantise_late(c)
+                if s == CHUNKS:
+                    floor_columns(0, B - 1)
                 if live(s - 1):
                     probabilities(s - 1)
-                if done[0] is not None:
-                    subtract_centres(done[0])
-                if done[3] is not None:
-                    invert_norms(done[3])
-                if done[5] is not None:
-                    scale_rows(done[5])
+                if s == CHUNKS:
+                    invert_columns(0, B - 1)
+                if batch_done:
+                    total_of_p(b)
                 if live(s - 2):
                     quantise_p(s - 2)
-                if live(s - 1):
-                    round_p(s - 1)
+                if s == CHUNKS:
+                    column_shares(0, B - 1)
+                if s == CHUNKS + 1:
+                    floor_rows(0, B - 1)
+                if batch_done:
+                    pooled_minus_centres(b)
                 for c in waiting:
                     quantise_late(c)
                 waiting = []
+                if live(s - 1):
+                    round_p(s - 1)
+                if s == CHUNKS:
+                    nc.scalar.sqrt(table_out[:], table_in[:])
+                if s == CHUNKS + 1:
+                    take_roots(0, B - 1)
                 if live(s):
                     exponentials(s)
-                if done[1] is not None:
-                    sum_of_squares(done[1])
-                if s >= 0 and done[0] is None and live(late_chunk):
+                if live(s + 3):
+                    normalise(s + 3)
+                if s == -2:
+                    nc.scalar.activation(out=table_out[:], in_=table_in[:], func=ACT.Exp)
+                if live(s - 4) and (s - 4) % CHUNKS_PER_BATCH == CHUNKS_PER_BATCH - 1:
+                    sum_of_squares((s - 4) // CHUNKS_PER_BATCH)
+                if s >= 0 and not batch_done and live(late_chunk):
                     if live(late_chunk + LATE_AHEAD):
                         load_late(late_chunk + LATE_AHEAD)
                     regroup_late(late_chunk, SCALAR_LATE)
                     waiting.append(late_chunk)
                     late_chunk += 1
-                if done[8] is not None:
-                    store(done[8])
-                if done[7] is not None:
-                    copy_out(done[7])
+            last = B - 1
+            whole = slice(0, D_BLOCKS)
+            halves = (slice(0, D_BLOCKS // 2), slice(D_BLOCKS // 2, D_BLOCKS))
+
+            def finish(b, copy):
+                copy_out(b, copy, whole)
+                store(b, whole)
+
+            pool_chunk(CHUNKS - 1)
+            invert_norms(0, last)
+            total_of_p(last)
+            for b in range(3):
+                scale_rows(b)
+                to_out(b)
+            pooled_minus_centres(last)
+            finish(0, nc.scalar.copy)
+            scale_rows(3)
+            to_out(3)
+            sum_of_squares(last)
+            finish(1, nc.scalar.copy)
+            scale_rows(4)
+            to_out(4)
+            finish(2, nc.scalar.copy)
+            floor_columns(last, B)
+            scale_rows(5)
+            to_out(5)
+            invert_columns(last, B)
+            finish(3, nc.scalar.copy)
+            scale_rows(6)
+            column_shares(last, B)
+            row_totals(last, B)
+            to_out(6)
+            floor_rows(last, B)
+            finish(4, nc.scalar.copy)
+            take_roots(last, B)
+            finish(5, nc.scalar.copy)
+            invert_norms(last, B)
+            scale_rows(last)
+            to_out(last)
+            finish(6, nc.vector.tensor_copy)
+            copy_out(last, nc.vector.tensor_copy, halves[0])
+            store(last, halves[0])
+            copy_out(last, nc.scalar.copy, halves[1])
+            store(last, halves[1])

@@ -27,6 +27,7 @@ D_EARLY = D - D_LATE
 D_CALL = 256
 SCALAR_D = 208
 SCALAR_LATE = 96
+RUN = 8
 LOAD_AHEAD = 4
 LATE_AHEAD = 5
 LATE_VECTOR = 2
@@ -124,12 +125,12 @@ def tile_modelnew_kernel(tc, x, clusters, clusters2, bn_gamma, bn_beta, out):
 
         def regroup_late(c, scalar_columns):
             g_late[c] = late.tile([P, D_LATE, PACK], BF16, align_bytes=64, name="g_late")
-            dst = g_late[c][:].rearrange("p (c i) j -> p c j i", i=4)
-            src = x_late[c][:].rearrange("p j (c i) -> p c j i", i=4)
-            cut = scalar_columns // 4
+            dst = g_late[c][:].rearrange("p (c i) j -> p c j i", i=RUN)
+            src = x_late[c][:].rearrange("p j (c i) -> p c j i", i=RUN)
+            cut = scalar_columns // RUN
             if cut > 0:
                 nc.scalar.copy(out=dst[:, 0:cut], in_=src[:, 0:cut])
-            if cut < D_LATE // 4:
+            if cut < D_LATE // RUN:
                 nc.vector.tensor_copy(out=dst[:, cut:], in_=src[:, cut:])
 
         def quantise_late(c):
@@ -226,9 +227,9 @@ def tile_modelnew_kernel(tc, x, clusters, clusters2, bn_gamma, bn_beta, out):
                 regroup_part(c, nc.vector)
 
             def regroup_part(c, engine):
-                dst = gn[c][:].rearrange("p (c i) j -> p c j i", i=4)
-                src = x_sb[c][:, :, 0:D_EARLY].rearrange("p j (c i) -> p c j i", i=4)
-                cut = SCALAR_D // 4
+                dst = gn[c][:].rearrange("p (c i) j -> p c j i", i=RUN)
+                src = x_sb[c][:, :, 0:D_EARLY].rearrange("p j (c i) -> p c j i", i=RUN)
+                cut = SCALAR_D // RUN
                 if engine is nc.scalar:
                     nc.scalar.copy(out=dst[:, 0:cut], in_=src[:, 0:cut])
                 else:
@@ -335,7 +336,10 @@ def tile_modelnew_kernel(tc, x, clusters, clusters2, bn_gamma, bn_beta, out):
 
             def round_p(c):
                 pg[c] = work.tile([P, K, PACK], BF16, align_bytes=64, name="pg")
-                nc.vector.tensor_copy(out=pg[c][:], in_=pf[c][:].rearrange("p j k -> p k j"))
+                nc.vector.tensor_copy(
+                    out=pg[c][:].rearrange("p (c i) j -> p c j i", i=4),
+                    in_=pf[c][:].rearrange("p j (c i) -> p c j i", i=4),
+                )
 
             def sum_of_p(c):
                 b, cc = divmod(c, CHUNKS_PER_BATCH)

@@ -30,7 +30,7 @@ SCALAR_LATE = 96
 RUN = 8
 LOAD_AHEAD = 4
 LATE_AHEAD = 5
-LATE_VECTOR = 2
+LATE_VECTOR = 4
 LATE_FILL = 6
 SETUP_STEP = 2
 
@@ -388,7 +388,7 @@ def tile_modelnew_kernel(tc, x, clusters, clusters2, bn_gamma, bn_beta, out):
                 )
 
             def sum_of_squares(b):
-                squares = outs.tile([P, D], F32, name="scaled")
+                squares = outs.tile([P, D], F32, name="scaled", bufs=5)
                 nc.scalar.activation(out=squares[:], in_=v[:, b, :], func=ACT.Square, accum_out=sumsq[:, b : b + 1])
 
             norm_sq, col_inv, share, norm, inv_norm = {}, {}, {}, {}, {}
@@ -428,7 +428,7 @@ def tile_modelnew_kernel(tc, x, clusters, clusters2, bn_gamma, bn_beta, out):
                     inv_norm[b] = inv[:, :, b - lo]
 
             def scale_rows(b):
-                scaled[b] = outs.tile([P, D], F32, name="scaled")
+                scaled[b] = outs.tile([P, D], F32, name="scaled", bufs=5)
                 nc.vector.tensor_scalar(
                     out=scaled[b][:],
                     in0=v[:, b, :],
@@ -439,21 +439,37 @@ def tile_modelnew_kernel(tc, x, clusters, clusters2, bn_gamma, bn_beta, out):
                 )
 
             def to_out(b):
-                oT[b] = ps_z.tile([P, D_BLOCKS, K], F32, name="z")
+                halves = 2 if b == B - 1 else 1
+                oT[b] = []
+                for h in range(halves):
+                    if (b + h) % 5 < 3:
+                        bank = ps_z.tile([P, D_BLOCKS, K], F32, name="z")
+                    else:
+                        bank = ps_a2.tile([P, D_BLOCKS, K], F32, name="aT")
+                    oT[b].append(bank)
                 for t in range(D_BLOCKS):
-                    nc.tensor.transpose(oT[b][:, t, :], scaled[b][:, t * P : (t + 1) * P], ident_f32[:])
+                    bank = oT[b][t * halves // D_BLOCKS]
+                    nc.tensor.transpose(bank[:, t, :], scaled[b][:, t * P : (t + 1) * P], ident_f32[:])
 
             def o_sb(b):
                 return v[:, b, :].rearrange("p (t k) -> p t k", t=D_BLOCKS)
 
-            def copy_out(b, copy, blocks):
-                copy(out=o_sb(b)[:, blocks, :], in_=oT[b][:, blocks, :])
+            def copy_out(b, copy):
+                if len(oT[b]) == 1:
+                    copy(out=o_sb(b), in_=oT[b][0][:])
+                else:
+                    half = D_BLOCKS // 2
+                    nc.vector.tensor_copy(out=o_sb(b)[:, :half, :], in_=oT[b][0][:, :half, :])
+                    nc.scalar.copy(out=o_sb(b)[:, half:, :], in_=oT[b][1][:, half:, :])
 
-            def store(b, blocks):
-                nc.sync.dma_start(
-                    out=out[b].rearrange("(t p k) -> p t k", t=D_BLOCKS, p=P)[:, blocks, :], in_=o_sb(b)[:, blocks, :]
-                )
+            def store(b):
+                rows = out[b].rearrange("(t p k) -> p t k", t=D_BLOCKS, p=P)
+                step = D_BLOCKS // len(oT[b])
+                for t in range(0, D_BLOCKS, step):
+                    nc.sync.dma_start(out=rows[:, t : t + step, :], in_=o_sb(b)[:, t : t + step, :])
 
+            last = B - 1
+            early = last - 1
             late_chunk = LATE_FILL + LATE_VECTOR
             waiting = []
             for c in range(LATE_FILL + LATE_VECTOR, LATE_FILL + LATE_VECTOR + LATE_AHEAD):
@@ -467,8 +483,10 @@ def tile_modelnew_kernel(tc, x, clusters, clusters2, bn_gamma, bn_beta, out):
                     pool_chunk(s - 3)
                 if live(s + 4):
                     project(ps_a2, s + 4)
+                if s == CHUNKS - 1:
+                    row_totals(0, early)
                 if s == CHUNKS + 1:
-                    row_totals(0, B - 1)
+                    row_totals(early, last)
                 if s >= 3 and live(s + 2):
                     to_rows(s + 2)
                 if live(s - 2):
@@ -483,20 +501,28 @@ def tile_modelnew_kernel(tc, x, clusters, clusters2, bn_gamma, bn_beta, out):
                 if s == 0:
                     for c in range(LATE_FILL + LATE_VECTOR):
                         quantise_late(c)
+                if s == CHUNKS - 2:
+                    floor_columns(0, early)
                 if s == CHUNKS:
-                    floor_columns(0, B - 1)
+                    floor_rows(0, early)
+                    floor_columns(early, last)
                 if live(s - 1):
                     probabilities(s - 1)
+                if s == CHUNKS - 2:
+                    invert_columns(0, early)
                 if s == CHUNKS:
-                    invert_columns(0, B - 1)
+                    invert_columns(early, last)
                 if batch_done:
                     total_of_p(b)
                 if live(s - 2):
                     quantise_p(s - 2)
+                if s == CHUNKS - 2:
+                    column_shares(0, early)
                 if s == CHUNKS:
-                    column_shares(0, B - 1)
+                    column_shares(early, last)
                 if s == CHUNKS + 1:
-                    floor_rows(0, B - 1)
+                    invert_norms(0, early)
+                    floor_rows(early, last)
                 if batch_done:
                     pooled_minus_centres(b)
                 for c in waiting:
@@ -506,8 +532,9 @@ def tile_modelnew_kernel(tc, x, clusters, clusters2, bn_gamma, bn_beta, out):
                     round_p(s - 1)
                 if s == CHUNKS:
                     nc.scalar.sqrt(table_out[:], table_in[:])
+                    take_roots(0, early)
                 if s == CHUNKS + 1:
-                    take_roots(0, B - 1)
+                    take_roots(early, last)
                 if live(s):
                     exponentials(s)
                 if live(s + 3):
@@ -522,47 +549,42 @@ def tile_modelnew_kernel(tc, x, clusters, clusters2, bn_gamma, bn_beta, out):
                     regroup_late(late_chunk, SCALAR_LATE)
                     waiting.append(late_chunk)
                     late_chunk += 1
-            last = B - 1
-            whole = slice(0, D_BLOCKS)
-            halves = (slice(0, D_BLOCKS // 2), slice(D_BLOCKS // 2, D_BLOCKS))
-
             def finish(b, copy):
-                copy_out(b, copy, whole)
-                store(b, whole)
+                copy_out(b, copy)
+                store(b)
 
             pool_chunk(CHUNKS - 1)
-            invert_norms(0, last)
-            total_of_p(last)
-            for b in range(3):
+            for b in range(2):
                 scale_rows(b)
                 to_out(b)
-            pooled_minus_centres(last)
+            total_of_p(last)
             finish(0, nc.scalar.copy)
+            scale_rows(2)
+            to_out(2)
+            pooled_minus_centres(last)
+            sum_of_squares(last)
             scale_rows(3)
             to_out(3)
-            sum_of_squares(last)
+            invert_norms(early, last)
             finish(1, nc.scalar.copy)
+            floor_columns(last, B)
             scale_rows(4)
             to_out(4)
-            finish(2, nc.scalar.copy)
-            floor_columns(last, B)
-            scale_rows(5)
-            to_out(5)
             invert_columns(last, B)
-            finish(3, nc.scalar.copy)
-            scale_rows(6)
+            scale_rows(5)
             column_shares(last, B)
             row_totals(last, B)
+            scale_rows(6)
+            finish(2, nc.scalar.copy)
+            to_out(5)
             to_out(6)
-            floor_rows(last, B)
             finish(4, nc.scalar.copy)
+            floor_rows(last, B)
             take_roots(last, B)
-            finish(5, nc.scalar.copy)
+            finish(3, nc.vector.tensor_copy)
             invert_norms(last, B)
             scale_rows(last)
+            finish(5, nc.scalar.copy)
+            finish(6, nc.scalar.copy)
             to_out(last)
-            finish(6, nc.vector.tensor_copy)
-            copy_out(last, nc.vector.tensor_copy, halves[0])
-            store(last, halves[0])
-            copy_out(last, nc.scalar.copy, halves[1])
-            store(last, halves[1])
+            finish(last, None)

@@ -26,7 +26,6 @@ D_LATE = 128
 D_EARLY = D - D_LATE
 D_CALL = 256
 SCALAR_D = 208
-SCALAR_LATE = 96
 RUN = 8
 LOAD_AHEAD = 4
 LATE_AHEAD = 5
@@ -295,6 +294,23 @@ def tile_modelnew_kernel(tc, x, clusters, clusters2, bn_gamma, bn_beta, out):
             s_odd = ps_s.tile([P, 4, P], F32, name="s_odd")
             s_bank = [s_even, s_odd]
 
+            moved = {}
+
+            def move_late(c, s):
+                g_late[c] = late.tile([P, D_LATE, PACK], BF16, align_bytes=64, name="g_late")
+                idle = s_bank[(s - 2 - CHUNKS_PER_BATCH) // CHUNKS_PER_BATCH % 2]
+                moved[c] = idle[:, 1:3, :].rearrange("p r k -> p (r k)").bitcast(BF16)
+                nc.tensor.matmul(
+                    out=moved[c],
+                    lhsT=ident_bf16[:],
+                    rhs=x_late[c][:].rearrange("p j d -> p d j"),
+                    start=True,
+                    stop=True,
+                )
+
+            def take_late(c):
+                nc.scalar.copy(out=g_late[c][:].rearrange("p d j -> p (d j)"), in_=moved[c])
+
             def normalise(c):
                 zT[c] = work.tile([P, K_PASS], F32, name="zT")
                 nc.scalar.activation(
@@ -477,6 +493,7 @@ def tile_modelnew_kernel(tc, x, clusters, clusters2, bn_gamma, bn_beta, out):
             for s in range(-LOAD_AHEAD, CHUNKS + 2):
                 b, cc = divmod(s - 3, CHUNKS_PER_BATCH)
                 batch_done = live(s - 3) and cc == CHUNKS_PER_BATCH - 1
+                late_now = late_chunk if s >= 0 and not batch_done and live(late_chunk) else None
                 if s < 3 and live(s + 2):
                     to_rows(s + 2)
                 if live(s - 3):
@@ -487,6 +504,8 @@ def tile_modelnew_kernel(tc, x, clusters, clusters2, bn_gamma, bn_beta, out):
                     row_totals(0, early)
                 if s == CHUNKS + 1:
                     row_totals(early, last)
+                if late_now is not None:
+                    move_late(late_now, s)
                 if s >= 3 and live(s + 2):
                     to_rows(s + 2)
                 if live(s - 2):
@@ -543,11 +562,11 @@ def tile_modelnew_kernel(tc, x, clusters, clusters2, bn_gamma, bn_beta, out):
                     nc.scalar.activation(out=table_out[:], in_=table_in[:], func=ACT.Exp)
                 if live(s - 4) and (s - 4) % CHUNKS_PER_BATCH == CHUNKS_PER_BATCH - 1:
                     sum_of_squares((s - 4) // CHUNKS_PER_BATCH)
-                if s >= 0 and not batch_done and live(late_chunk):
-                    if live(late_chunk + LATE_AHEAD):
-                        load_late(late_chunk + LATE_AHEAD)
-                    regroup_late(late_chunk, SCALAR_LATE)
-                    waiting.append(late_chunk)
+                if late_now is not None:
+                    if live(late_now + LATE_AHEAD):
+                        load_late(late_now + LATE_AHEAD)
+                    take_late(late_now)
+                    waiting.append(late_now)
                     late_chunk += 1
             def finish(b, copy):
                 copy_out(b, copy)

from contextlib import ExitStack

import concourse.mybir as mybir
from concourse.masks import make_identity

F32 = mybir.dt.float32
BF16 = mybir.dt.bfloat16
U32 = mybir.dt.uint32
U8 = mybir.dt.uint8
FP8X4 = mybir.dt.float8_e4m3fn_x4
ALU = mybir.AluOpType
ACT = mybir.ActivationFunctionType
AX = mybir.AxisListType

P = 128
PACK = 4
K_PASS = P * PACK
B, N, D, K = 8, 2048, 512, 128
ROWS = B * N
CHUNKS = ROWS // K_PASS
CHUNKS_PER_BATCH = N // K_PASS
D_BLOCKS = D // P
BN_EPS = 1e-5
NORM_EPS = 1e-12
D_LATE = 128
D_EARLY = D - D_LATE
D_CALL = 256
SCALAR_D = 208
RUN = 8
LOAD_AHEAD = 4
LATE_AHEAD = 5
LATE_VECTOR = 4
LATE_FILL = 6
SETUP_STEP = 2

FLOPS = 2 * 2 * ROWS * D * K


def live(c):
    return 0 <= c < CHUNKS


def tile_modelnew_kernel(tc, x, clusters, clusters2, bn_gamma, bn_beta, out):
    nc = tc.nc
    x_rows = x.flatten_outer_dims()

    with ExitStack() as ctx:
        ctx.enter_context(tc.manual_schedule())
        keep = ctx.enter_context(tc.tile_pool(name="keep", bufs=1))
        late = ctx.enter_context(tc.tile_pool(name="late", bufs=LATE_FILL + LATE_VECTOR + 1))

        ident_f32 = keep.tile([P, P], F32)
        make_identity(nc, ident_f32[:])
        ident_bf16 = keep.tile([P, P], BF16)
        make_identity(nc, ident_bf16[:])
        ones_f32 = keep.tile([P, P], F32)
        nc.vector.memset(ones_f32[:], 1.0)
        table_in = keep.tile([P, 1], F32)
        nc.vector.memset(table_in[:], 1.0)
        table_out = keep.tile([P, 1], F32)
        eps = keep.tile([P, 1], F32)
        nc.vector.tensor_scalar(
            out=eps[:], in0=table_in[:], scalar1=0.0, scalar2=BN_EPS, op0=ALU.mult, op1=ALU.add
        )

        cl_sb = keep.tile([P, PACK, K], BF16)
        for u in range(2):
            nc.scalar.dma_start(
                out=cl_sb[:, 2 * u : 2 * u + 2, :],
                in_=clusters[256 * u : 256 * u + 256, :].rearrange("(q e) k -> q e k", e=2),
            )
        nc.scalar.sqrt(table_out[:], table_in[:])

        c2_sb = keep.tile([P, D_BLOCKS, K], BF16)
        gb_rows = keep.tile([P, P], BF16)
        nc.vector.memset(gb_rows[:], 0.0)

        def load_small_inputs():
            nc.sync.dma_start(out=c2_sb[:], in_=clusters2[0].rearrange("(t p) k -> p t k", p=P))
            nc.sync.dma_start(out=gb_rows[0:1, :], in_=bn_gamma.rearrange("(o k) -> o k", o=1))
            nc.sync.dma_start(out=gb_rows[1:2, :], in_=bn_beta.rearrange("(o k) -> o k", o=1))

        cl_grouped = keep.tile([P, K, PACK], BF16, align_bytes=64)
        cl_codes = keep.tile([P, K], U32, align_bytes=64)
        cl_scales = keep.tile([P, K], U8, align_bytes=64)

        def quantise_clusters():
            nc.vector.tensor_copy(out=cl_grouped[:], in_=cl_sb[:].rearrange("q t k -> q k t"))
            nc.vector.quantize_mx(
                out=cl_codes[:].bitcast(FP8X4),
                scales=cl_scales[:],
                in_=cl_grouped[:].rearrange("q k t -> q (k t)"),
            )

        c2T = keep.tile([P, D], F32)
        gb = keep.tile([P, 2], F32)

        xd_codes = keep.tile([P, CHUNKS, K_PASS], U32, align_bytes=64)
        xd_scales = keep.tile([P, CHUNKS, K_PASS], U8, align_bytes=64)
        xn_codes = keep.tile([P, CHUNKS, D], U32, align_bytes=64)
        xn_scales = keep.tile([P, CHUNKS, D], U8, align_bytes=64)
        stats = keep.tile([P, CHUNKS, 6], F32)
        aT = {}
        x_late, g_late = {}, {}

        def project(psum, c):
            aT[c] = psum.tile([P, K_PASS], F32, name="aT")
            nc.tensor.matmul_mx(
                out=aT[c][:],
                lhsT=cl_codes[:].bitcast(FP8X4),
                lhsT_scale=cl_scales[:],
                rhs=xd_codes[:, c, :].bitcast(FP8X4),
                rhs_scale=xd_scales[:, c, :],
                start=True,
                stop=True,
            )

        def load_late(c):
            x_late[c] = late.tile([P, PACK, D_LATE], BF16, name="x_late", bufs=6)
            nc.sync.dma_start(
                out=x_late[c][:],
                in_=x_rows[c * K_PASS : (c + 1) * K_PASS, D_EARLY:D].rearrange("(p j) d -> p j d", j=PACK),
            )

        def regroup_late(c, scalar_columns):
            g_late[c] = late.tile([P, D_LATE, PACK], BF16, align_bytes=64, name="g_late")
            dst = g_late[c][:].rearrange("p (c i) j -> p c j i", i=RUN)
            src = x_late[c][:].rearrange("p j (c i) -> p c j i", i=RUN)
            cut = scalar_columns // RUN
            if cut > 0:
                nc.scalar.copy(out=dst[:, 0:cut], in_=src[:, 0:cut])
            if cut < D_LATE // RUN:
                nc.vector.tensor_copy(out=dst[:, cut:], in_=src[:, cut:])

        def quantise_late(c):
            nc.vector.quantize_mx(
                out=xn_codes[:, c, D_EARLY:D].bitcast(FP8X4),
                scales=xn_scales[:, c, D_EARLY:D],
                in_=g_late[c][:].rearrange("p d j -> p (d j)"),
            )

        mean_var = keep.tile([P, 2], F32)
        std = keep.tile([P, 1], F32)
        neg_mean = keep.tile([P, 1], F32)
        rstd = keep.tile([P, 1], F32)
        bn_scale = keep.tile([P, 1], F32)
        bn_shift = keep.tile([P, 1], F32)

        def batch_norm_vectors():
            nc.vector.bn_aggr(out=mean_var[:], in_=stats[:].rearrange("p c s -> p (c s)"))
            nc.scalar.activation(out=std[:], in_=mean_var[:, 1:2], func=ACT.Sqrt, bias=eps[:, 0:1], scale=1.0)
            nc.vector.tensor_scalar_mul(out=neg_mean[:], in0=mean_var[:, 0:1], scalar1=-1.0)
            nc.vector.reciprocal(rstd[:], std[:])
            nc.vector.tensor_mul(out=bn_scale[:], in0=gb[:, 0:1], in1=rstd[:])
            nc.vector.scalar_tensor_tensor(
                out=bn_shift[:], in0=neg_mean[:], scalar=bn_scale[:, 0:1], in1=gb[:, 1:2], op0=ALU.mult, op1=ALU.add
            )

        with ExitStack() as ph1:
            xin = ph1.enter_context(tc.tile_pool(name="xin", bufs=LOAD_AHEAD + 2))
            grp = ph1.enter_context(tc.tile_pool(name="grp", bufs=3))
            grn = ph1.enter_context(tc.tile_pool(name="grn", bufs=4))
            ps_set = ph1.enter_context(tc.psum_pool(name="ps_set", bufs=1))
            ps_xt = ph1.enter_context(tc.psum_pool(name="ps_xt", bufs=4))
            ps_a1 = ph1.enter_context(tc.psum_pool(name="ps_a1", bufs=2))
            x_sb, xt, gd, gn = {}, {}, {}, {}

            def transpose_small_inputs():
                c2T_ps = ps_set.tile([P, D_BLOCKS, P], BF16)
                for t in range(D_BLOCKS):
                    nc.tensor.transpose(c2T_ps[:, t, :], c2_sb[:, t, :], ident_bf16[:])
                nc.vector.tensor_copy(out=c2T[:], in_=c2T_ps[:].rearrange("k t p -> k (t p)"))
                gb_ps = ps_set.tile([P, P], BF16)
                nc.tensor.transpose(gb_ps[:], gb_rows[:], ident_bf16[:])
                nc.vector.tensor_copy(out=gb[:], in_=gb_ps[:, 0:2])

            def load(c):
                x_sb[c] = xin.tile([P, PACK, D], BF16, name="x_sb")
                src = x_rows[c * K_PASS : (c + 1) * K_PASS, :].rearrange("(p j) d -> p j d", j=PACK)
                pieces = 2 if c == 0 else 1
                rows = PACK // pieces
                for i in range(pieces):
                    nc.sync.dma_start(
                        out=x_sb[c][:, i * rows : (i + 1) * rows, :], in_=src[:, i * rows : (i + 1) * rows, :]
                    )

            def transpose_words(c):
                x_words = x_sb[c][:].bitcast(F32)
                xt[c] = []
                for h in range(2):
                    bank = ps_xt.tile([P, 2, 2 * P], F32, name="xt")
                    for u in range(2):
                        for jj in range(2):
                            nc.tensor.transpose(
                                bank[:, u, jj * P : (jj + 1) * P],
                                x_words[:, 2 * h + jj, u * P : (u + 1) * P],
                                ident_f32[:],
                            )
                    xt[c].append(bank)

            def copy_words(c):
                gd[c] = grp.tile([P, K_PASS, PACK], BF16, align_bytes=64, name="gd")
                gd_words = gd[c][:].bitcast(F32)
                for h in range(2):
                    nc.scalar.copy(
                        out=gd_words[:, h * 2 * P : (h + 1) * 2 * P, :],
                        in_=xt[c][h][:].rearrange("q u n -> q n u"),
                    )

            def quantise_along_d(c):
                nc.vector.quantize_mx(
                    out=xd_codes[:, c, :].bitcast(FP8X4),
                    scales=xd_scales[:, c, :],
                    in_=gd[c][:].rearrange("q n t -> q (n t)"),
                )

            def regroup(c):
                scalar_part(c)
                vector_part(c)

            def scalar_part(c):
                gn[c] = grn.tile([P, D_EARLY, PACK], BF16, align_bytes=64, name="gn")
                regroup_part(c, nc.scalar)

            def vector_part(c):
                regroup_part(c, nc.vector)

            def regroup_part(c, engine):
                dst = gn[c][:].rearrange("p (c i) j -> p c j i", i=RUN)
                src = x_sb[c][:, :, 0:D_EARLY].rearrange("p j (c i) -> p c j i", i=RUN)
                cut = SCALAR_D // RUN
                if engine is nc.scalar:
                    nc.scalar.copy(out=dst[:, 0:cut], in_=src[:, 0:cut])
                else:
                    nc.vector.tensor_copy(out=dst[:, cut:], in_=src[:, cut:])

            def quantise_along_n(c):
                for cols in (slice(0, D_CALL), slice(D_CALL, D_EARLY)):
                    nc.vector.quantize_mx(
                        out=xn_codes[:, c, cols].bitcast(FP8X4),
                        scales=xn_scales[:, c, cols],
                        in_=gn[c][:, cols, :].rearrange("p d j -> p (d j)"),
                    )

            def statistics(c):
                nc.vector.bn_stats(out=stats[:, c, :], in_=aT[c][:])

            for s in range(-LOAD_AHEAD, CHUNKS + 2):
                if live(s + LOAD_AHEAD):
                    load(s + LOAD_AHEAD)
                if s == -1:
                    load_small_inputs()
                if CHUNKS <= s + LOAD_AHEAD < CHUNKS + (LATE_FILL + LATE_VECTOR) // 2:
                    load_late(2 * (s + LOAD_AHEAD - CHUNKS))
                    load_late(2 * (s + LOAD_AHEAD - CHUNKS) + 1)
                if live(s + 1):
                    transpose_words(s + 1)
                if s == SETUP_STEP:
                    transpose_small_inputs()
                if s == 0:
                    quantise_clusters()
                if live(s - 1):
                    quantise_along_d(s - 1)
                    project(ps_a1, s - 1)
                if live(s):
                    copy_words(s)
                    if s < CHUNKS - 1:
                        regroup(s)
                if live(s - 1) and s - 1 < CHUNKS - 3:
                    quantise_along_n(s - 1)
                if live(s - 2):
                    statistics(s - 2)
            scalar_part(CHUNKS - 1)
            for c in range(LATE_FILL):
                regroup_late(c, D_LATE)
            batch_norm_vectors()
            vector_part(CHUNKS - 1)
            for c in range(CHUNKS - 3, CHUNKS):
                quantise_along_n(c)

        with ExitStack() as ph2:
            work = ph2.enter_context(tc.tile_pool(name="work", bufs=3))
            outs = ph2.enter_context(tc.tile_pool(name="outs", bufs=3))
            norms = ph2.enter_context(tc.tile_pool(name="norms", bufs=2))
            ps_a2 = ph2.enter_context(tc.psum_pool(name="ps_a2", bufs=2))
            ps_z = ph2.enter_context(tc.psum_pool(name="ps_z", bufs=3))
            ps_v = ph2.enter_context(tc.psum_pool(name="ps_v", bufs=1))
            ps_s = ph2.enter_context(tc.psum_pool(name="ps_s", bufs=1))
            zT, z, neg_max, e, row_sum, inv_sum, pf, pg, p_codes, p_scales, vT = {}, {}, {}, {}, {}, {}, {}, {}, {}, {}, {}
            scaled, oT, neg_asum = {}, {}, {}
            v = outs.tile([P, B, D], F32, bufs=1)
            sumsq = norms.tile([P, B], F32, bufs=1)
            s_even = ps_s.tile([P, 4, P], F32, name="s_even")
            s_odd = ps_s.tile([P, 4, P], F32, name="s_odd")
            s_bank = [s_even, s_odd]

            moved = {}

            def move_late(c, s):
                g_late[c] = late.tile([P, D_LATE, PACK], BF16, align_bytes=64, name="g_late")
                idle = s_bank[(s - 2 - CHUNKS_PER_BATCH) // CHUNKS_PER_BATCH % 2]
                moved[c] = idle[:, 1:3, :].rearrange("p r k -> p (r k)").bitcast(BF16)
                nc.tensor.matmul(
                    out=moved[c],
                    lhsT=ident_bf16[:],
                    rhs=x_late[c][:].rearrange("p j d -> p d j"),
                    start=True,
                    stop=True,
                )

            def take_late(c):
                nc.scalar.copy(out=g_late[c][:].rearrange("p d j -> p (d j)"), in_=moved[c])

            def normalise(c):
                zT[c] = work.tile([P, K_PASS], F32, name="zT")
                nc.scalar.activation(
                    out=zT[c][:], in_=aT[c][:], func=ACT.Identity, scale=bn_scale[:, 0:1], bias=bn_shift[:, 0:1]
                )

            def to_rows(c):
                z[c] = ps_z.tile([P, PACK, K], F32, name="z")
                for j in range(PACK):
                    nc.tensor.transpose(z[c][:, j, :], zT[c][:, j * P : (j + 1) * P], ident_f32[:])

            def row_max(c):
                neg_max[c] = work.tile([P, PACK], F32, name="neg_max")
                nc.vector.tensor_reduce(out=neg_max[c][:], in_=z[c][:], axis=AX.X, op=ALU.max, negate=True)

            def exponentials(c):
                e[c] = work.tile([P, PACK, K], F32, name="e")
                row_sum[c] = work.tile([P, PACK], F32, name="row_sum")
                for j in range(PACK):
                    nc.scalar.activation(
                        out=e[c][:, j, :],
                        in_=z[c][:, j, :],
                        func=ACT.Exp,
                        bias=neg_max[c][:, j : j + 1],
                        scale=1.0,
                        accum_out=row_sum[c][:, j : j + 1],
                    )

            def invert_sums(c):
                inv_sum[c] = work.tile([P, PACK], F32, name="inv_sum")
                nc.vector.reciprocal(inv_sum[c][:], row_sum[c][:])

            def probabilities(c):
                pf[c] = work.tile([P, PACK, K], F32, name="pf")
                for j in range(PACK):
                    nc.vector.tensor_scalar_mul(
                        out=pf[c][:, j, :], in0=e[c][:, j, :], scalar1=inv_sum[c][:, j : j + 1]
                    )

            def round_p(c):
                pg[c] = work.tile([P, K, PACK], BF16, align_bytes=64, name="pg")
                nc.vector.tensor_copy(
                    out=pg[c][:].rearrange("p (c i) j -> p c j i", i=4),
                    in_=pf[c][:].rearrange("p j (c i) -> p c j i", i=4),
                )

            def sum_of_p(c):
                b, cc = divmod(c, CHUNKS_PER_BATCH)
                for j in range(PACK):
                    nc.tensor.matmul(
                        out=s_bank[b % 2][:, 0, :],
                        lhsT=pf[c][:, j, :],
                        rhs=ident_f32[:],
                        is_transpose=True,
                        start=(cc == 0 and j == 0),
                        stop=(cc == CHUNKS_PER_BATCH - 1 and j == PACK - 1),
                    )

            def quantise_p(c):
                p_codes[c] = work.tile([P, K], U32, align_bytes=64, name="p_codes")
                p_scales[c] = work.tile([P, K], U8, align_bytes=64, name="p_scales")
                nc.vector.quantize_mx(
                    out=p_codes[c][:].bitcast(FP8X4),
                    scales=p_scales[c][:],
                    in_=pg[c][:].rearrange("p k j -> p (k j)"),
                )

            def pool_chunk(c):
                b, cc = divmod(c, CHUNKS_PER_BATCH)
                if cc == 0:
                    vT[b] = ps_v.tile([P, D], F32, name="vT")
                nc.tensor.matmul_mx(
                    out=vT[b][:],
                    lhsT=p_codes[c][:].bitcast(FP8X4),
                    lhsT_scale=p_scales[c][:],
                    rhs=xn_codes[:, c, :].bitcast(FP8X4),
                    rhs_scale=xn_scales[:, c, :],
                    start=(cc == 0),
                    stop=(cc == CHUNKS_PER_BATCH - 1),
                )

            def total_of_p(b):
                neg_asum[b] = norms.tile([P, 1], F32, name="neg_asum")
                nc.vector.tensor_reduce(
                    out=neg_asum[b][:], in_=s_bank[b % 2][:, 0, :], axis=AX.X, op=ALU.add, negate=True
                )

            def pooled_minus_centres(b):
                nc.vector.scalar_tensor_tensor(
                    out=v[:, b, :], in0=c2T[:], scalar=neg_asum[b][:, 0:1], in1=vT[b][:], op0=ALU.mult, op1=ALU.add
                )

            def sum_of_squares(b):
                squares = outs.tile([P, D], F32, name="scaled", bufs=5)
                nc.scalar.activation(out=squares[:], in_=v[:, b, :], func=ACT.Square, accum_out=sumsq[:, b : b + 1])

            norm_sq, col_inv, share, norm, inv_norm = {}, {}, {}, {}, {}

            def floor_columns(lo, hi):
                norm_sq[lo] = norms.tile([P, 2, hi - lo], F32, name="norm_sq%d" % lo)
                nc.vector.tensor_scalar_max(
                    out=norm_sq[lo][:, 0, :], in0=sumsq[:, lo:hi], scalar1=NORM_EPS * NORM_EPS
                )

            def invert_columns(lo, hi):
                col_inv[lo] = norms.tile([P, hi - lo], F32, name="col_inv%d" % lo)
                nc.vector.reciprocal(col_inv[lo][:], norm_sq[lo][:, 0, :])

            def column_shares(lo, hi):
                share[lo] = norms.tile([P, hi - lo], F32, name="share%d" % lo)
                nc.vector.tensor_mul(out=share[lo][:], in0=sumsq[:, lo:hi], in1=col_inv[lo][:])

            def row_totals(lo, hi):
                nc.tensor.matmul(
                    out=s_bank[0][:, 1, lo:hi], lhsT=ones_f32[:], rhs=share[lo][:], start=True, stop=True
                )

            def floor_rows(lo, hi):
                nc.vector.tensor_scalar_max(
                    out=norm_sq[lo][:, 1, :], in0=s_bank[0][:, 1, lo:hi], scalar1=NORM_EPS * NORM_EPS
                )

            def take_roots(lo, hi):
                norm[lo] = norms.tile([P, 2, hi - lo], F32, name="norm%d" % lo)
                nc.scalar.sqrt(norm[lo][:], norm_sq[lo][:])

            def invert_norms(lo, hi):
                inv = norms.tile([P, 2, hi - lo], F32, name="inv_norm%d" % lo)
                nc.vector.reciprocal(inv[:], norm[lo][:])
                for b in range(lo, hi):
                    inv_norm[b] = inv[:, :, b - lo]

            def scale_rows(b):
                scaled[b] = outs.tile([P, D], F32, name="scaled", bufs=5)
                nc.vector.tensor_scalar(
                    out=scaled[b][:],
                    in0=v[:, b, :],
                    scalar1=inv_norm[b][:, 0:1],
                    scalar2=inv_norm[b][:, 1:2],
                    op0=ALU.mult,
                    op1=ALU.mult,
                )

            def to_out(b):
                halves = 2 if b == B - 1 else 1
                oT[b] = []
                for h in range(halves):
                    if (b + h) % 5 < 3:
                        bank = ps_z.tile([P, D_BLOCKS, K], F32, name="z")
                    else:
                        bank = ps_a2.tile([P, D_BLOCKS, K], F32, name="aT")
                    oT[b].append(bank)
                for t in range(D_BLOCKS):
                    bank = oT[b][t * halves // D_BLOCKS]
                    nc.tensor.transpose(bank[:, t, :], scaled[b][:, t * P : (t + 1) * P], ident_f32[:])

            def o_sb(b):
                return v[:, b, :].rearrange("p (t k) -> p t k", t=D_BLOCKS)

            def copy_out(b, copy):
                if len(oT[b]) == 1:
                    copy(out=o_sb(b), in_=oT[b][0][:])
                else:
                    half = D_BLOCKS // 2
                    nc.vector.tensor_copy(out=o_sb(b)[:, :half, :], in_=oT[b][0][:, :half, :])
                    nc.scalar.copy(out=o_sb(b)[:, half:, :], in_=oT[b][1][:, half:, :])

            def store(b):
                rows = out[b].rearrange("(t p k) -> p t k", t=D_BLOCKS, p=P)
                step = D_BLOCKS // len(oT[b])
                for t in range(0, D_BLOCKS, step):
                    nc.sync.dma_start(out=rows[:, t : t + step, :], in_=o_sb(b)[:, t : t + step, :])

            last = B - 1
            early = last - 1
            late_chunk = LATE_FILL + LATE_VECTOR
            waiting = []
            for c in range(LATE_FILL + LATE_VECTOR, LATE_FILL + LATE_VECTOR + LATE_AHEAD):
                load_late(c)
            for s in range(-LOAD_AHEAD, CHUNKS + 2):
                b, cc = divmod(s - 3, CHUNKS_PER_BATCH)
                batch_done = live(s - 3) and cc == CHUNKS_PER_BATCH - 1
                late_now = late_chunk if s >= 0 and not batch_done and live(late_chunk) else None
                if s < 3 and live(s + 2):
                    to_rows(s + 2)
                if live(s - 3):
                    pool_chunk(s - 3)
                if live(s + 4):
                    project(ps_a2, s + 4)
                if s == CHUNKS - 1:
                    row_totals(0, early)
                if s == CHUNKS + 1:
                    row_totals(early, last)
                if late_now is not None:
                    move_late(late_now, s)
                if s >= 3 and live(s + 2):
                    to_rows(s + 2)
                if live(s - 2):
                    sum_of_p(s - 2)
                if live(s - 1):
                    invert_sums(s - 1)
                if live(s + 1):
                    row_max(s + 1)
                if s == -1:
                    for c in range(LATE_FILL, LATE_FILL + LATE_VECTOR):
                        regroup_late(c, 0)
                if s == 0:
                    for c in range(LATE_FILL + LATE_VECTOR):
                        quantise_late(c)
                if s == CHUNKS - 2:
                    floor_columns(0, early)
                if s == CHUNKS:
                    floor_rows(0, early)
                    floor_columns(early, last)
                if live(s - 1):
                    probabilities(s - 1)
                if s == CHUNKS - 2:
                    invert_columns(0, early)
                if s == CHUNKS:
                    invert_columns(early, last)
                if batch_done:
                    total_of_p(b)
                if live(s - 2):
                    quantise_p(s - 2)
                if s == CHUNKS - 2:
                    column_shares(0, early)
                if s == CHUNKS:
                    column_shares(early, last)
                if s == CHUNKS + 1:
                    invert_norms(0, early)
                    floor_rows(early, last)
                if batch_done:
                    pooled_minus_centres(b)
                for c in waiting:
                    quantise_late(c)
                waiting = []
                if live(s - 1):
                    round_p(s - 1)
                if s == CHUNKS:
                    nc.scalar.sqrt(table_out[:], table_in[:])
                    take_roots(0, early)
                if s == CHUNKS + 1:
                    take_roots(early, last)
                if live(s):
                    exponentials(s)
                if live(s + 3):
                    normalise(s + 3)
                if s == -2:
                    nc.scalar.activation(out=table_out[:], in_=table_in[:], func=ACT.Exp)
                if live(s - 4) and (s - 4) % CHUNKS_PER_BATCH == CHUNKS_PER_BATCH - 1:
                    sum_of_squares((s - 4) // CHUNKS_PER_BATCH)
                if late_now is not None:
                    if live(late_now + LATE_AHEAD):
                        load_late(late_now + LATE_AHEAD)
                    take_late(late_now)
                    waiting.append(late_now)
                    late_chunk += 1
            def finish(b, copy):
                copy_out(b, copy)
                store(b)

            pool_chunk(CHUNKS - 1)
            for b in range(2):
                scale_rows(b)
                to_out(b)
            total_of_p(last)
            finish(0, nc.scalar.copy)
            scale_rows(2)
            to_out(2)
            pooled_minus_centres(last)
            sum_of_squares(last)
            scale_rows(3)
            to_out(3)
            invert_norms(early, last)
            finish(1, nc.scalar.copy)
            floor_columns(last, B)
            scale_rows(4)
            to_out(4)
            invert_columns(last, B)
            scale_rows(5)
            column_shares(last, B)
            row_totals(last, B)
            scale_rows(6)
            finish(2, nc.scalar.copy)
            to_out(5)
            to_out(6)
            finish(4, nc.scalar.copy)
            floor_rows(last, B)
            take_roots(last, B)
            finish(3, nc.vector.tensor_copy)
            invert_norms(last, B)
            scale_rows(last)
            finish(5, nc.scalar.copy)
            finish(6, nc.scalar.copy)
            to_out(last)
            finish(last, None)
